import numpy as np
import ml_dtypes


def mxq(x, axis, fmt="e4m3"):
    dtype, down = {"e4m3": (ml_dtypes.float8_e4m3fn, 7), "e5m2": (ml_dtypes.float8_e5m2, 14)}[fmt]
    v = np.moveaxis(np.asarray(x, np.float32).astype(ml_dtypes.bfloat16).astype(np.float64), axis, -1)
    blocks = v.reshape(v.shape[:-1] + (-1, 32))
    amax = np.abs(blocks).max(-1, keepdims=True)
    byte = np.maximum(np.where(amax > 0, np.frexp(amax)[1] - 1 + 127, 0) - down, 1)
    scale = np.exp2(byte - 127.0)
    codes = (blocks / scale).astype(np.float32).astype(dtype).astype(np.float64)
    return np.moveaxis((codes * scale).reshape(v.shape), -1, axis)


WIDE = False


def mx_kscale(k):
    if not WIDE:
        return np.ones(k)
    levels = np.array([10, -10, 5, -5, 0])
    if k % 512:
        return np.exp2(np.random.permutation(np.resize(levels, k // 32))).repeat(32)
    a = np.empty((k // 512, 16))
    for p in range(k // 512):
        a[p, :8] = np.random.permutation(np.resize(levels, 8))
        for g in range(8):
            far = levels[np.abs(levels - a[p, g]) >= 10]
            a[p, g + 8] = far[np.random.randint(len(far))]
    return np.exp2(a.ravel()).repeat(32)


BF16 = ml_dtypes.bfloat16


def bf(x):
    return np.asarray(x, np.float32).astype(BF16)


def f64(x):
    return np.asarray(x).astype(np.float64)


B, S, E, H, C = 1, 512, 2048, 16, 512
HD = E // H
EPS = 1e-5


def silu(v):
    return v / (1.0 + np.exp(-v))


def setup_inputs():
    s, t = mx_kscale(E), mx_kscale(E)
    spread = np.exp(0.7 * np.random.standard_normal((B, S, H, 1)))
    shift = 0.5 * np.random.standard_normal((B, S, H, 1))
    attn = 1.5 * (np.random.standard_normal((B, S, H, HD)) * spread + shift)
    return {"x": bf(np.random.standard_normal((B, S, E)) * s),
            "attn": bf(attn.reshape(B, S, E)),
            "Wg": bf(np.random.standard_normal((E, E)) / np.sqrt(E) / s[:, None]),
            "bg": bf(np.random.standard_normal(E) * 0.2),
            "gn_w": bf((1.0 + 0.1 * np.random.standard_normal(E)) * t),
            "gn_b": bf(0.1 * np.random.standard_normal(E) * t),
            "Wo": bf(np.random.standard_normal((E, E)) * 1.5 / np.sqrt(E) / t[:, None]),
            "bo": bf(np.random.standard_normal(E) * 0.1)}


def reference(x, attn, Wg, bg, gn_w, gn_b, Wo, bo):
    g = f64(attn).reshape(B, S, H, HD)
    mu = g.mean(-1, keepdims=True)
    var = g.var(-1, keepdims=True)
    g = (g - mu) / np.sqrt(var + EPS)
    g = g.reshape(B, S, E) * f64(gn_w) + f64(gn_b)
    gate = silu((mxq(f64(x), 2, "e4m3") @ mxq(f64(Wg), 0, "e4m3")) + f64(bg))
    h = gate * g
    return (mxq(h, 2, "e4m3") @ mxq(f64(Wo), 0, "e4m3")) + f64(bo)

@@ -1,0 +1,355 @@
+from contextlib import ExitStack
+
+import concourse.mybir as mybir
+from concourse.masks import make_identity
+
+F32 = mybir.dt.float32
+BF16 = mybir.dt.bfloat16
+U32 = mybir.dt.uint32
+U8 = mybir.dt.uint8
+FP8X4 = mybir.dt.float8_e4m3fn_x4
+ALU = mybir.AluOpType
+ACT = mybir.ActivationFunctionType
+
+P = 128
+S = 512
+E = 2048
+EPS = 1e-5
+NPASS = E // 512
+FLOPS = 2 * 2 * S * E * E
+
+ORDER = [
+    ("ldA", 0), ("ld", "g", 0, 0), ("ldA", 1), ("bn", 0), ("ld", "g", 0, 1), ("RGS", "g", 0, 0),
+    ("RGV", "g", 1, 0), ("ldA", 2), ("Q", "g", 1, 0), ("bn", 1), ("ld", "g", 0, 2), ("RGS", "g", 0, 1),
+    ("Q", "g", 0, 0), ("ldA", 3), ("bn", 2), ("ld", "g", 0, 3), ("RGS", "g", 1, 1), ("Q", "g", 0, 1),
+    ("RGV", "g", 0, 2), ("RGS", "g", 1, 2), ("ld", "x", 0, 0), ("bn", 3), ("ld", "x", 1, 0), ("sm",),
+    ("RGS", "g", 0, 3), ("Q", "g", 0, 2), ("Q", "g", 1, 1), ("Q", "g", 1, 2), ("ld", "g", 1, 0), ("sqrt",),
+    ("RGV", "g", 1, 3), ("xT", 0, 0), ("xT", 1, 0), ("recip",), ("Q", "g", 0, 3), ("XE", 0, 0), ("xT", 2, 0),
+    ("J4", 0, 0), ("XE", 1, 0), ("xT", 3, 0), ("J4", 0, 1), ("ld", "g", 1, 1), ("XE", 2, 0), ("J4", 0, 2),
+    ("xT", 0, 1), ("J4", 0, 3), ("XE", 3, 0), ("xT", 1, 1), ("Q", "g", 1, 3), ("XE", 0, 1), ("xT", 2, 1),
+    ("J4", 1, 0), ("XE", 1, 1), ("xT", 3, 1), ("J4", 1, 1), ("ld", "g", 1, 2), ("Qx", 0), ("XE", 2, 1),
+    ("T", 0, 0), ("Qx", 1), ("XE", 3, 1), ("T", 0, 1), ("Qx", 2), ("GW", 0, 0), ("T", 0, 2), ("Qx", 3),
+    ("GW", 0, 1), ("T", 0, 3), ("RGV", "g", 2, 0), ("ld", "g", 1, 3), ("GW", 0, 2), ("GW", 0, 3),
+    ("MX1", 0, 0), ("J4", 1, 2), ("RGS", "g", 2, 1), ("J4", 1, 3), ("Q", "g", 2, 0), ("MX1", 0, 1),
+    ("J4", 2, 0), ("ldbo",), ("RGV", "g", 2, 2), ("MX1", 0, 2), ("SIL", 0, 0), ("ld", "o", 0, 0),
+    ("Q", "g", 2, 1), ("SIL", 0, 1), ("MX1", 0, 3), ("Q", "g", 2, 2), ("RGS", "g", 3, 1), ("J4", 2, 1),
+    ("RGV", "g", 3, 0), ("T", 1, 0), ("ld", "o", 0, 1), ("T", 1, 1), ("Q", "g", 3, 0), ("SIL", 0, 2),
+    ("T", 1, 2), ("RGV", "g", 3, 2), ("SIL", 0, 3), ("T", 1, 3), ("GW", 1, 0), ("MX1", 1, 0),
+    ("Q", "g", 3, 1), ("ld", "o", 0, 2), ("GW", 1, 1), ("MUL", 0), ("GW", 1, 2), ("MX1", 1, 1), ("GW", 1, 3),
+    ("SIL", 1, 0), ("MX1", 1, 2), ("SIL", 1, 1), ("ld", "o", 0, 3), ("QH", 0), ("RGS", "g", 2, 3),
+    ("MX1", 1, 3), ("J4", 2, 2), ("J4", 2, 3), ("Q", "g", 3, 2), ("T", 2, 0), ("RGV", "g", 3, 3),
+    ("ld", "o", 1, 0), ("T", 2, 1), ("SIL", 1, 2), ("Q", "g", 3, 3), ("T", 2, 2), ("SIL", 1, 3),
+    ("Q", "g", 2, 3), ("T", 2, 3), ("GW", 2, 0), ("J4", 3, 0), ("GW", 2, 1), ("MX1", 3, 0), ("MUL", 1),
+    ("ld", "o", 1, 1), ("GW", 2, 2), ("GW", 2, 3), ("MX1", 2, 0), ("SIL", 3, 0), ("QH", 1),
+    ("RGS", "o", 0, 2), ("MX1", 2, 1), ("J4", 3, 1), ("J4", 3, 2), ("MX1", 2, 2), ("J4", 3, 3),
+    ("RGV", "o", 0, 0), ("SIL", 2, 0), ("MX1", 2, 3), ("SIL", 2, 1), ("Q", "o", 0, 0), ("SIL", 2, 2),
+    ("RGV", "o", 0, 1), ("T", 3, 0), ("RGS", "o", 0, 3), ("T", 3, 1), ("Q", "o", 0, 1), ("T", 3, 2),
+    ("Q", "o", 0, 2), ("T", 3, 3), ("RGV", "o", 1, 0), ("MX1", 3, 1), ("SIL", 2, 3), ("GW", 3, 0),
+    ("Q", "o", 0, 3), ("MX1", 3, 2), ("ld", "o", 1, 2), ("GW", 3, 1), ("MUL", 2), ("GW", 3, 2), ("MX1", 3, 3),
+    ("GW", 3, 3), ("SIL", 3, 1), ("QH", 2), ("MX2", 0, 0), ("SIL", 3, 2), ("Q", "o", 1, 0), ("SIL", 3, 3),
+    ("RGV", "o", 1, 3), ("MX2", 0, 1), ("RGS", "o", 1, 1), ("MUL", 3), ("MX2", 0, 2), ("ld", "o", 1, 3),
+    ("RGS", "o", 1, 2), ("MX2", 1, 0), ("QH", 3), ("Q", "o", 1, 1), ("Q", "o", 1, 3), ("RGS", "o", 2, 0),
+    ("MX2", 0, 3), ("RGV", "o", 2, 2), ("MX2", 1, 1), ("Q", "o", 1, 2), ("J5", 0, 0), ("RGS", "o", 2, 1),
+    ("J5", 0, 1), ("MX2", 1, 2), ("st", 0, 0), ("J5", 0, 2), ("J5", 0, 3), ("st", 0, 1), ("MX2", 1, 3),
+    ("RGS", "o", 3, 0), ("Q", "o", 2, 0), ("st", 0, 2), ("Q", "o", 2, 1), ("st", 0, 3), ("Q", "o", 2, 2),
+    ("MX2", 2, 0), ("RGV", "o", 2, 3), ("RGS", "o", 3, 1), ("MX2", 2, 1), ("Q", "o", 2, 3), ("J5", 1, 0),
+    ("MX2", 2, 2), ("J5", 1, 1), ("RGS", "o", 3, 3), ("st", 1, 0), ("J5", 1, 2), ("J5", 1, 3), ("st", 1, 1),
+    ("MX2", 2, 3), ("Q", "o", 3, 0), ("st", 1, 2), ("Q", "o", 3, 1), ("st", 1, 3), ("RGV", "o", 3, 2),
+    ("MX2", 3, 0), ("Q", "o", 3, 2), ("MX2", 3, 1), ("Q", "o", 3, 3), ("J5", 2, 0), ("MX2", 3, 2),
+    ("J5", 2, 1), ("st", 2, 0), ("J5", 2, 2), ("J5", 2, 3), ("st", 2, 1), ("MX2", 3, 3), ("st", 2, 2),
+    ("st", 2, 3), ("J5", 3, 0), ("J5", 3, 1), ("st", 3, 0), ("J5", 3, 2), ("st", 3, 1), ("J5", 3, 3),
+    ("st", 3, 2), ("st", 3, 3),
+]
+
+
+def tile_multiscaleretention_pb_kernel(tc, x, attn, Wg, bg, gn_w, gn_b, Wo, bo, out):
+    nc = tc.nc
+    xf = x.flatten_outer_dims()
+    af = attn.flatten_outer_dims()
+    of = out.flatten_outer_dims()
+
+    with ExitStack() as ctx:
+        const = ctx.enter_context(tc.tile_pool(name="const", bufs=1))
+        rawp = ctx.enter_context(tc.tile_pool(name="rawp", bufs=6))
+        grpp = ctx.enter_context(tc.tile_pool(name="grpp", bufs=5))
+        codep = ctx.enter_context(tc.tile_pool(name="codep", bufs=6))
+        normp = ctx.enter_context(tc.tile_pool(name="normp", bufs=6))
+        gatep = ctx.enter_context(tc.tile_pool(name="gatep", bufs=2))
+        outp = ctx.enter_context(tc.tile_pool(name="outp", bufs=6))
+        psum = ctx.enter_context(tc.psum_pool(name="psum", bufs=8))
+
+
+        ident = const.tile([P, P], F32, name="ident")
+        make_identity(nc, ident[:])
+        vraw = const.tile([P, 512], BF16, name="vraw")
+        nc.vector.memset(vraw[:], 0.0)
+        eps_t = const.tile([P, 1], F32, name="eps_t")
+        nc.vector.memset(eps_t[:], EPS)
+        nc.scalar.dma_start(out=vraw[0:4, :], in_=bg.rearrange("(r c) -> r c", c=512))
+        nc.scalar.dma_start(out=vraw[4:8, :], in_=gn_w.rearrange("(r c) -> r c", c=512))
+        nc.scalar.dma_start(out=vraw[8:12, :], in_=gn_b.rearrange("(r c) -> r c", c=512))
+        warm = const.tile([P, 1], F32, name="warm")
+        nc.scalar.activation(out=warm[:], in_=eps_t[:], func=ACT.Sqrt, scale=1.0)
+
+        bo_bc = const.tile([P, E], BF16, name="bo_bc")
+        vf = const.tile([P, 512], F32, name="vf")
+        vcol = const.tile([P, 4, 12], F32, name="vcol")
+        st = const.tile([P, 64, 6], F32, name="st")
+        dif = const.tile([P, 64], F32, name="dif")
+        mu = const.tile([P, 64], F32, name="mu")
+        m2 = const.tile([P, 64], F32, name="m2")
+        std = const.tile([P, 64], F32, name="std")
+        rstd = const.tile([P, 64], F32, name="rstd")
+        xc = const.tile([P, NPASS, S], U32, name="xc", align_bytes=64)
+        xs = const.tile([P, NPASS, S], U8, name="xs", align_bytes=64)
+        hc = const.tile([P, NPASS, S], U32, name="hc", align_bytes=64)
+        hs = const.tile([P, NPASS, S], U8, name="hs", align_bytes=64)
+        T = {}
+
+        def ld_attn(s):
+            T[("a", s)] = const.tile([P, E], BF16, name="a_sb%d" % s)
+            cuts = 2 if s == 0 else 1
+            w = E // cuts
+            for i in range(cuts):
+                nc.sync.dma_start(out=T[("a", s)][:, w * i:w * i + w], in_=af[P * s:P * s + P, w * i:w * i + w])
+
+        def ld_raw(kind, a, c):
+            t = rawp.tile([P, 4096], BF16, name="raw_%s%d%d" % (kind, a, c), tag="raw")
+            T[("raw", kind, a, c)] = t
+            if kind == "x":
+                nc.sync.dma_start(
+                    out=t[:].rearrange("p (s k) -> p s k", s=2),
+                    in_=xf[256 * a:256 * a + 256, :].rearrange("(s p) k -> p s k", p=P),
+                )
+            elif kind == "g":
+                tv = t[:].rearrange("p (t c) -> p t c", t=4)
+                cuts = 2 if (a == 0 and c == 0) else 1
+                w = 1024 // cuts
+                for i in range(cuts):
+                    c0 = 1024 * a + w * i
+                    nc.sync.dma_start(
+                        out=tv[:, :, w * i:w * i + w],
+                        in_=Wg[512 * c:512 * c + 512, c0:c0 + w].rearrange("(p j) c -> p j c", j=4),
+                    )
+            else:
+                nc.sync.dma_start(
+                    out=t[:].rearrange("p (t c) -> p t c", t=4),
+                    in_=Wo[512 * c:512 * c + 512, 1024 * a:1024 * a + 1024].rearrange("(p t) c -> p t c", t=4),
+                )
+
+        def vec_prep():
+            nc.vector.tensor_copy(
+                out=vf[:].rearrange("p (t m) -> p t m", t=4), in_=vraw[:].rearrange("p (m t) -> p t m", t=4)
+            )
+            vt = psum.tile([P, 4, P], F32, name="vt", tag="ps")
+            for t in range(4):
+                nc.tensor.transpose(vt[:, t, :], vf[:, P * t:P * t + P], ident[:])
+            nc.vector.tensor_copy(out=vcol[:], in_=vt[:, :, 0:12])
+
+        def bn(s):
+            for g in range(16):
+                nc.vector.bn_stats(out=st[:, 16 * s + g, :], in_=T[("a", s)][:, P * g:P * g + P])
+            if s == 0:
+                vec_prep()
+
+        def small():
+            me, m2e, mo, m2o = st[:, :, 1], st[:, :, 2], st[:, :, 4], st[:, :, 5]
+            nc.vector.tensor_tensor(out=dif[:], in0=me, in1=mo, op=ALU.subtract)
+            nc.vector.tensor_tensor(out=mu[:], in0=me, in1=mo, op=ALU.add)
+            nc.vector.tensor_tensor(out=m2[:], in0=m2e, in1=m2o, op=ALU.add)
+            nc.vector.tensor_tensor(out=dif[:], in0=dif[:], in1=dif[:], op=ALU.mult)
+            nc.vector.tensor_scalar(out=mu[:], in0=mu[:], scalar1=0.5, scalar2=None, op0=ALU.mult)
+            nc.vector.scalar_tensor_tensor(
+                out=m2[:], in0=dif[:], scalar=32.0, in1=m2[:], op0=ALU.mult, op1=ALU.add
+            )
+
+        def x_transpose(g, sp):
+            xt = psum.tile([P, 2, 256], F32, name="xt%d%d" % (g, sp), tag="ps")
+            T[("xt", g, sp)] = xt
+            xw = T[("raw", "x", sp, 0)][:].bitcast(F32)
+            for u in range(2):
+                for sl in range(2):
+                    c0 = 1024 * sl + 256 * g
+                    nc.tensor.transpose(xt[:, u, P * sl:P * sl + P], xw[:, c0 + u:c0 + 256:2], ident[:])
+
+        def x_evac(g, sp):
+            if ("xq", g) not in T:
+                T[("xq", g)] = grpp.tile([P, 2048], BF16, name="xq%d" % g, tag="grp", align_bytes=64)
+            xq32 = T[("xq", g)][:].bitcast(F32).rearrange("p (r u) -> p r u", u=2)
+            nc.scalar.copy(
+                out=xq32[:, 256 * sp:256 * sp + 256, :], in_=T[("xt", g, sp)][:].rearrange("p u r -> p r u")
+            )
+
+        def regroup(eng, kind, blk, c):
+            raw = T[("raw", kind, blk // 2, c)]
+            col0 = 512 * (blk % 2)
+            src = raw[:].rearrange("p (t c) -> p t c", t=4)[:, :, col0:col0 + 512]
+            g4 = grpp.tile([P, 2048], BF16, name="g4_%s%d%d" % (kind, blk, c), tag="grp", align_bytes=64)
+            T[("g4", kind, blk, c)] = g4
+            if kind == "g":
+                dst = g4[:].rearrange("p (t m j) -> p t m j", t=4, j=4)
+                srcv = src.rearrange("p j (m t) -> p t m j", t=4)
+            else:
+                dst = g4[:].rearrange("p (c i t) -> p c t i", i=4, t=4)
+                srcv = src.rearrange("p t (c i) -> p c t i", i=4)
+            if eng == "V":
+                nc.vector.tensor_copy(out=dst, in_=srcv)
+            else:
+                nc.scalar.copy(out=dst, in_=srcv)
+
+        def quant(kind, blk, c):
+            if ("wc", kind, blk) not in T:
+                T[("wc", kind, blk)] = codep.tile(
+                    [P, NPASS, 512], U32, name="wc_%s%d" % (kind, blk), tag="wc", align_bytes=64
+                )
+                T[("ws", kind, blk)] = codep.tile(
+                    [P, NPASS, 512], U8, name="ws_%s%d" % (kind, blk), tag="ws", align_bytes=64
+                )
+            nc.vector.quantize_mx(
+                out=T[("wc", kind, blk)][:, c, :].bitcast(FP8X4),
+                scales=T[("ws", kind, blk)][:, c, :],
+                in_=T[("g4", kind, blk, c)][:],
+            )
+
+        def mx1(G, t):
+            z = psum.tile([P, S], F32, name="z%d%d" % (G, t), tag="ps")
+            T[("z", G, t)] = z
+            wc, ws = T[("wc", "g", G)], T[("ws", "g", G)]
+            for c in range(NPASS):
+                nc.tensor.matmul_mx(
+                    out=z[:],
+                    lhsT=wc[:, c, P * t:P * t + P].bitcast(FP8X4),
+                    lhsT_scale=ws[:, c, P * t:P * t + P],
+                    rhs=xc[:, c, :].bitcast(FP8X4),
+                    rhs_scale=xs[:, c, :],
+                    start=(c == 0),
+                    stop=(c == NPASS - 1),
+                )
+
+        def normalise(G, s):
+            nrm = normp.tile([P, 512], F32, name="nrm%d%d" % (G, s), tag="nrm")
+            T[("nrm", G, s)] = nrm
+            for t in range(4):
+                gi = 4 * G + t
+                k = 16 * s + gi
+                nc.vector.tensor_scalar(
+                    out=nrm[:].rearrange("p (t m) -> p t m", t=4)[:, :, 32 * t:32 * t + 32],
+                    in0=T[("a", s)][:, P * gi:P * gi + P].rearrange("p (m t) -> p t m", t=4),
+                    scalar1=mu[:, k:k + 1],
+                    scalar2=rstd[:, k:k + 1],
+                    op0=ALU.subtract,
+                    op1=ALU.mult,
+                )
+
+        def n_transpose(G, t):
+            nT = psum.tile([P, S], F32, name="nT%d%d" % (G, t), tag="ps")
+            T[("nT", G, t)] = nT
+            for s in range(4):
+                nc.tensor.transpose(nT[:, P * s:P * s + P], T[("nrm", G, s)][:, P * t:P * t + P], ident[:])
+
+        def silu(G, t):
+            if ("sil", G) not in T:
+                T[("sil", G)] = gatep.tile([P, 2048], F32, name="sil%d" % G, tag="sil")
+            nc.scalar.activation(
+                out=T[("sil", G)][:, S * t:S * t + S], in_=T[("z", G, t)][:], func=ACT.Silu,
+                bias=vcol[:, t, G:G + 1], scale=1.0,
+            )
+
+        def gain(G, t):
+            if ("gw", G) not in T:
+                T[("gw", G)] = gatep.tile([P, 2048], F32, name="gw%d" % G, tag="gw")
+            nc.scalar.activation(
+                out=T[("gw", G)][:, S * t:S * t + S], in_=T[("nT", G, t)][:], func=ACT.Identity,
+                bias=vcol[:, t, 8 + G:9 + G], scale=vcol[:, t, 4 + G:5 + G],
+            )
+
+        def gate_mul(G):
+            hq = grpp.tile([P, 2048], BF16, name="hq%d" % G, tag="grp", align_bytes=64)
+            T[("hq", G)] = hq
+            nc.vector.tensor_tensor(
+                out=hq[:].rearrange("p (c i t) -> p c t i", i=4, t=4),
+                in0=T[("sil", G)][:].rearrange("p (t c i) -> p c t i", t=4, i=4),
+                in1=T[("gw", G)][:].rearrange("p (t c i) -> p c t i", t=4, i=4),
+                op=ALU.mult,
+            )
+
+        def mx2(NB, G):
+            if G == 0:
+                for s in range(4):
+                    T[("acc", NB, s)] = psum.tile(
+                        [P, 512], F32, name="acc%d%d" % (NB, s), tag="ps"
+                    )
+            wc, ws = T[("wc", "o", NB)], T[("ws", "o", NB)]
+            for s in range(4):
+                nc.tensor.matmul_mx(
+                    out=T[("acc", NB, s)][:],
+                    lhsT=hc[:, G, P * s:P * s + P].bitcast(FP8X4),
+                    lhsT_scale=hs[:, G, P * s:P * s + P],
+                    rhs=wc[:, G, :].bitcast(FP8X4),
+                    rhs_scale=ws[:, G, :],
+                    start=(G == 0),
+                    stop=(G == NPASS - 1),
+                )
+
+        def bias_out(NB, s):
+            o_sb = outp.tile([P, 512], F32, name="o%d%d" % (NB, s), tag="o")
+            T[("o", NB, s)] = o_sb
+            nc.vector.tensor_tensor(
+                out=o_sb[:], in0=T[("acc", NB, s)][:], in1=bo_bc[:, 512 * NB:512 * NB + 512], op=ALU.add
+            )
+
+        for tok in ORDER:
+            k = tok[0]
+            if k == "ldA":
+                ld_attn(tok[1])
+            elif k == "ld":
+                ld_raw(tok[1], tok[2], tok[3])
+            elif k == "ldbo":
+                nc.sync.dma_start(out=bo_bc[:], in_=bo.partition_broadcast(P))
+            elif k == "bn":
+                bn(tok[1])
+            elif k == "sm":
+                small()
+            elif k == "sqrt":
+                nc.scalar.activation(out=std[:], in_=m2[:], func=ACT.Sqrt, bias=eps_t[:, 0:1], scale=1.0 / P)
+            elif k == "recip":
+                nc.vector.reciprocal(out=rstd[:], in_=std[:])
+            elif k == "xT":
+                x_transpose(tok[1], tok[2])
+            elif k == "XE":
+                x_evac(tok[1], tok[2])
+            elif k == "Qx":
+                nc.vector.quantize_mx(
+                    out=xc[:, tok[1], :].bitcast(FP8X4), scales=xs[:, tok[1], :], in_=T[("xq", tok[1])][:]
+                )
+            elif k == "RGV":
+                regroup("V", tok[1], tok[2], tok[3])
+            elif k == "RGS":
+                regroup("S", tok[1], tok[2], tok[3])
+            elif k == "Q":
+                quant(tok[1], tok[2], tok[3])
+            elif k == "MX1":
+                mx1(tok[1], tok[2])
+            elif k == "J4":
+                normalise(tok[1], tok[2])
+            elif k == "T":
+                n_transpose(tok[1], tok[2])
+            elif k == "SIL":
+                silu(tok[1], tok[2])
+            elif k == "GW":
+                gain(tok[1], tok[2])
+            elif k == "MUL":
+                gate_mul(tok[1])
+            elif k == "QH":
+                nc.vector.quantize_mx(
+                    out=hc[:, tok[1], :].bitcast(FP8X4), scales=hs[:, tok[1], :], in_=T[("hq", tok[1])][:]
+                )
+            elif k == "MX2":
+                mx2(tok[1], tok[2])
+            elif k == "J5":
+                bias_out(tok[1], tok[2])
+            elif k == "st":
+                NB, s = tok[1], tok[2]
+                nc.sync.dma_start(out=of[P * s:P * s + P, 512 * NB:512 * NB + 512], in_=T[("o", NB, s)][:])
+            else:
+                assert False, k

@@ -187,8 +187,8 @@ def tile_multiscaleretention_pb_kernel(tc, x, attn, Wg, bg, gn_w, gn_b, Wo, bo, 
             g4 = grpp.tile([P, 2048], BF16, name="g4_%s%d%d" % (kind, blk, c), tag="grp", align_bytes=64)
             T[("g4", kind, blk, c)] = g4
             if kind == "g":
-                dst = g4[:].rearrange("p (t m j) -> p t m j", t=4, j=4)
-                srcv = src.rearrange("p j (m t) -> p t m j", t=4)
+                dst = g4[:].rearrange("p (t m j) -> p m j t", t=4, j=4)
+                srcv = src.rearrange("p j (m t) -> p m j t", t=4)
             else:
                 dst = g4[:].rearrange("p (c i t) -> p c t i", i=4, t=4)
                 srcv = src.rearrange("p t (c i) -> p c t i", i=4)
@@ -233,8 +233,8 @@ def tile_multiscaleretention_pb_kernel(tc, x, attn, Wg, bg, gn_w, gn_b, Wo, bo, 
                 gi = 4 * G + t
                 k = 16 * s + gi
                 nc.vector.tensor_scalar(
-                    out=nrm[:].rearrange("p (t m) -> p t m", t=4)[:, :, 32 * t:32 * t + 32],
-                    in0=T[("a", s)][:, P * gi:P * gi + P].rearrange("p (m t) -> p t m", t=4),
+                    out=nrm[:].rearrange("p (t m) -> p m t", t=4)[:, 32 * t:32 * t + 32, :],
+                    in0=T[("a", s)][:, P * gi:P * gi + P].rearrange("p (m t) -> p m t", t=4),
                     scalar1=mu[:, k:k + 1],
                     scalar2=rstd[:, k:k + 1],
                     op0=ALU.subtract,

@@ -233,8 +233,8 @@ def tile_multiscaleretention_pb_kernel(tc, x, attn, Wg, bg, gn_w, gn_b, Wo, bo, 
                 gi = 4 * G + t
                 k = 16 * s + gi
                 nc.vector.tensor_scalar(
-                    out=nrm[:].rearrange("p (t m) -> p m t", t=4)[:, 32 * t:32 * t + 32, :],
-                    in0=T[("a", s)][:, P * gi:P * gi + P].rearrange("p (m t) -> p m t", t=4),
+                    out=nrm[:].rearrange("p (t m) -> p t m", t=4)[:, :, 32 * t:32 * t + 32],
+                    in0=T[("a", s)][:, P * gi:P * gi + P].rearrange("p (m t) -> p t m", t=4),
                     scalar1=mu[:, k:k + 1],
                     scalar2=rstd[:, k:k + 1],
                     op0=ALU.subtract,

@@ -18,48 +18,85 @@ EPS = 1e-5
 NPASS = E // 512
 FLOPS = 2 * 2 * S * E * E
 
-ORDER = [
-    ("ldA", 0), ("ld", "g", 0, 0), ("ldA", 1), ("bn", 0), ("ld", "g", 0, 1), ("RGS", "g", 0, 0),
-    ("RGV", "g", 1, 0), ("ldA", 2), ("Q", "g", 1, 0), ("bn", 1), ("ld", "g", 0, 2), ("RGS", "g", 0, 1),
-    ("Q", "g", 0, 0), ("ldA", 3), ("bn", 2), ("ld", "g", 0, 3), ("RGS", "g", 1, 1), ("Q", "g", 0, 1),
-    ("RGV", "g", 0, 2), ("RGS", "g", 1, 2), ("ld", "x", 0, 0), ("bn", 3), ("ld", "x", 1, 0), ("sm",),
-    ("RGS", "g", 0, 3), ("Q", "g", 0, 2), ("Q", "g", 1, 1), ("Q", "g", 1, 2), ("ld", "g", 1, 0), ("sqrt",),
-    ("RGV", "g", 1, 3), ("xT", 0, 0), ("xT", 1, 0), ("recip",), ("Q", "g", 0, 3), ("XE", 0, 0), ("xT", 2, 0),
-    ("J4", 0, 0), ("XE", 1, 0), ("xT", 3, 0), ("J4", 0, 1), ("ld", "g", 1, 1), ("XE", 2, 0), ("J4", 0, 2),
-    ("xT", 0, 1), ("J4", 0, 3), ("XE", 3, 0), ("xT", 1, 1), ("Q", "g", 1, 3), ("XE", 0, 1), ("xT", 2, 1),
-    ("J4", 1, 0), ("XE", 1, 1), ("xT", 3, 1), ("J4", 1, 1), ("ld", "g", 1, 2), ("Qx", 0), ("XE", 2, 1),
-    ("T", 0, 0), ("Qx", 1), ("XE", 3, 1), ("T", 0, 1), ("Qx", 2), ("GW", 0, 0), ("T", 0, 2), ("Qx", 3),
-    ("GW", 0, 1), ("T", 0, 3), ("RGV", "g", 2, 0), ("ld", "g", 1, 3), ("GW", 0, 2), ("GW", 0, 3),
-    ("MX1", 0, 0), ("J4", 1, 2), ("RGS", "g", 2, 1), ("J4", 1, 3), ("Q", "g", 2, 0), ("MX1", 0, 1),
-    ("J4", 2, 0), ("ldbo",), ("RGV", "g", 2, 2), ("MX1", 0, 2), ("SIL", 0, 0), ("ld", "o", 0, 0),
-    ("Q", "g", 2, 1), ("SIL", 0, 1), ("MX1", 0, 3), ("Q", "g", 2, 2), ("RGS", "g", 3, 1), ("J4", 2, 1),
-    ("RGV", "g", 3, 0), ("T", 1, 0), ("ld", "o", 0, 1), ("T", 1, 1), ("Q", "g", 3, 0), ("SIL", 0, 2),
-    ("T", 1, 2), ("RGV", "g", 3, 2), ("SIL", 0, 3), ("T", 1, 3), ("GW", 1, 0), ("MX1", 1, 0),
-    ("Q", "g", 3, 1), ("ld", "o", 0, 2), ("GW", 1, 1), ("MUL", 0), ("GW", 1, 2), ("MX1", 1, 1), ("GW", 1, 3),
-    ("SIL", 1, 0), ("MX1", 1, 2), ("SIL", 1, 1), ("ld", "o", 0, 3), ("QH", 0), ("RGS", "g", 2, 3),
-    ("MX1", 1, 3), ("J4", 2, 2), ("J4", 2, 3), ("Q", "g", 3, 2), ("T", 2, 0), ("RGV", "g", 3, 3),
-    ("ld", "o", 1, 0), ("T", 2, 1), ("SIL", 1, 2), ("Q", "g", 3, 3), ("T", 2, 2), ("SIL", 1, 3),
-    ("Q", "g", 2, 3), ("T", 2, 3), ("GW", 2, 0), ("J4", 3, 0), ("GW", 2, 1), ("MX1", 3, 0), ("MUL", 1),
-    ("ld", "o", 1, 1), ("GW", 2, 2), ("GW", 2, 3), ("MX1", 2, 0), ("SIL", 3, 0), ("QH", 1),
-    ("RGS", "o", 0, 2), ("MX1", 2, 1), ("J4", 3, 1), ("J4", 3, 2), ("MX1", 2, 2), ("J4", 3, 3),
-    ("RGV", "o", 0, 0), ("SIL", 2, 0), ("MX1", 2, 3), ("SIL", 2, 1), ("Q", "o", 0, 0), ("SIL", 2, 2),
-    ("RGV", "o", 0, 1), ("T", 3, 0), ("RGS", "o", 0, 3), ("T", 3, 1), ("Q", "o", 0, 1), ("T", 3, 2),
-    ("Q", "o", 0, 2), ("T", 3, 3), ("RGV", "o", 1, 0), ("MX1", 3, 1), ("SIL", 2, 3), ("GW", 3, 0),
-    ("Q", "o", 0, 3), ("MX1", 3, 2), ("ld", "o", 1, 2), ("GW", 3, 1), ("MUL", 2), ("GW", 3, 2), ("MX1", 3, 3),
-    ("GW", 3, 3), ("SIL", 3, 1), ("QH", 2), ("MX2", 0, 0), ("SIL", 3, 2), ("Q", "o", 1, 0), ("SIL", 3, 3),
-    ("RGV", "o", 1, 3), ("MX2", 0, 1), ("RGS", "o", 1, 1), ("MUL", 3), ("MX2", 0, 2), ("ld", "o", 1, 3),
-    ("RGS", "o", 1, 2), ("MX2", 1, 0), ("QH", 3), ("Q", "o", 1, 1), ("Q", "o", 1, 3), ("RGS", "o", 2, 0),
-    ("MX2", 0, 3), ("RGV", "o", 2, 2), ("MX2", 1, 1), ("Q", "o", 1, 2), ("J5", 0, 0), ("RGS", "o", 2, 1),
-    ("J5", 0, 1), ("MX2", 1, 2), ("st", 0, 0), ("J5", 0, 2), ("J5", 0, 3), ("st", 0, 1), ("MX2", 1, 3),
-    ("RGS", "o", 3, 0), ("Q", "o", 2, 0), ("st", 0, 2), ("Q", "o", 2, 1), ("st", 0, 3), ("Q", "o", 2, 2),
-    ("MX2", 2, 0), ("RGV", "o", 2, 3), ("RGS", "o", 3, 1), ("MX2", 2, 1), ("Q", "o", 2, 3), ("J5", 1, 0),
-    ("MX2", 2, 2), ("J5", 1, 1), ("RGS", "o", 3, 3), ("st", 1, 0), ("J5", 1, 2), ("J5", 1, 3), ("st", 1, 1),
-    ("MX2", 2, 3), ("Q", "o", 3, 0), ("st", 1, 2), ("Q", "o", 3, 1), ("st", 1, 3), ("RGV", "o", 3, 2),
-    ("MX2", 3, 0), ("Q", "o", 3, 2), ("MX2", 3, 1), ("Q", "o", 3, 3), ("J5", 2, 0), ("MX2", 3, 2),
-    ("J5", 2, 1), ("st", 2, 0), ("J5", 2, 2), ("J5", 2, 3), ("st", 2, 1), ("MX2", 3, 3), ("st", 2, 2),
-    ("st", 2, 3), ("J5", 3, 0), ("J5", 3, 1), ("st", 3, 0), ("J5", 3, 2), ("st", 3, 1), ("J5", 3, 3),
-    ("st", 3, 2), ("st", 3, 3),
-]
+SA = [("g", 2, 0), ("g", 3, 0), ("g", 2, 2), ("g", 2, 3), ("g", 3, 2), ("g", 3, 3), ("o", 0, 1), ("o", 1, 0), ("o", 1, 2), ("o", 2, 0), ("o", 2, 2), ("o", 3, 0), ("o", 3, 2)]
+SV = [("g", 2, 1), ("g", 3, 1), ("o", 0, 0), ("o", 0, 2), ("o", 0, 3), ("o", 1, 1), ("o", 1, 3), ("o", 2, 1), ("o", 3, 1), ("o", 2, 3), ("o", 3, 3)]
+CA = (2, 2, 2, 1)
+CV = (2, 3, 2, 2)
+
+def needs(t):
+    k = t[0]
+    if k == "bn": return [("ldA", t[1])]
+    if k == "sm": return [("bn", s) for s in range(4)]
+    if k == "sqrt": return [("sm",)]
+    if k == "recip": return [("sqrt",)]
+    if k == "xT": return [("ld", "x", t[2], 0)]
+    if k == "XE": return [("xT",) + t[1:]]
+    if k == "Qx": return [("XE", t[1], 0), ("XE", t[1], 1)]
+    if k in ("RGV", "RGS"): return [("ld", t[1], t[2] // 2, t[3])]
+    if k == "Q": return [("RG",) + t[1:]]
+    if k == "J4": return [("recip",)]
+    if k == "T": return [("J4", t[1], s) for s in range(4)]
+    if k == "GW": return [("T",) + t[1:]]
+    if k == "MX1": return [("Q", "g", t[1], c) for c in range(4)] + [("Qx", c) for c in range(4)]
+    if k == "SIL": return [("MX1",) + t[1:]]
+    if k == "MUL": return [("SIL", t[1], 3), ("GW", t[1], 3)]
+    if k == "QH": return [("MUL", t[1])]
+    if k == "MX2": return [("QH", t[2]), ("Q", "o", t[1], t[2])]
+    if k == "J5": return [("MX2", t[1], 3), ("ldbo",)]
+    if k == "st": return [("J5",) + t[1:]]
+    return []
+
+def pipeline():
+    D, V, A, PE = [], [], [], []
+    for i in range(2):
+        D += [("ldA", 0, 2 * i, 4), ("ldA", 0, 2 * i + 1, 4), ("ld", "g", 0, 0, i, 2)]
+    for c in range(1, 4):
+        D += [("ldA", c), ("ld", "g", 0, c)]
+    D += [("ld", "x", sp, 0) for sp in range(2)]
+    D += [("ld", "g", 1, c) for c in range(4)] + [("ldbo",)]
+    D += [("ld", "o", a, c) for a in range(2) for c in range(4)]
+    D += [("st", NB, s) for NB in range(4) for s in range(4)]
+    A += [("RGS", "g", 0, 0), ("RGS", "g", 0, 1), ("RGS", "g", 1, 1), ("RGS", "g", 0, 2), ("RGS", "g", 0, 3)]
+    A += [("XE", g, 0) for g in range(4)] + [("XE", 0, 1), ("XE", 1, 1), ("sqrt",), ("XE", 2, 1), ("XE", 3, 1)]
+    sa = list(SA)
+    for G in range(4):
+        for i in range(CA[G]): A.append(("RGS",) + sa.pop(0))
+        A += [("GW", G, t) for t in range(4)] + [("SIL", G, t) for t in range(4)]
+    A += [("RGS",) + u for u in sa]
+    PE += [("xT", g, sp) for sp in range(2) for g in range(4)]
+    PE += [("T", 0, t) for t in range(4)]
+    for G in range(4):
+        PE += [("MX1", G, t) for t in range(4)]
+        if G < 3: PE += [("T", G + 1, t) for t in range(4)]
+    PE += [("MX2", NB, G) for NB in range(4) for G in range(4)]
+    q = lambda kind, b, c: ("Q", kind, b, c)
+    V += [("bn", 0), ("RGV", "g", 1, 0), ("bn", 1), q("g", 0, 0), q("g", 1, 0), ("bn", 2), q("g", 0, 1), q("g", 1, 1), ("RGV", "g", 1, 2)]
+    V += [("bn", 3), q("g", 0, 2), q("g", 1, 2), ("RGV", "g", 1, 3), ("sm",), q("g", 0, 3), q("g", 1, 3), ("Qx", 0), ("recip",), ("Qx", 1), ("Qx", 2), ("Qx", 3)]
+    V += [("J4", 0, s) for s in range(4)]
+    V += [q("g", 2, 0), ("RGV",) + SV[0], ("J4", 1, 0), q("g", 2, 1), ("J4", 1, 1), ("J4", 1, 2), ("J4", 1, 3), q("g", 3, 0), ("RGV",) + SV[1], ("J4", 2, 0), q("g", 3, 1)]
+    V += [("J4", 2, s) for s in range(1, 4)]
+    V += [("MUL", 0), q("g", 2, 2), ("QH", 0), ("RGV",) + SV[2], q("g", 2, 3), q(*SV[2]), ("RGV",) + SV[3], ("RGV",) + SV[4], q(*SV[3]), q(*SV[4])]
+    V += [("MUL", 1), q("g", 3, 2), ("QH", 1)] + [("J4", 3, s) for s in range(2)] + [q("g", 3, 3)] + [("J4", 3, s) for s in range(2, 4)]
+    V += [("RGV",) + SV[5], ("RGV",) + SV[6], q(*SV[5]), q(*SV[6]), ("MUL", 2), q("o", 0, 1), ("QH", 2), ("RGV",) + SV[7], ("RGV",) + SV[8], q(*SV[7]), q(*SV[8])]
+    V += [("MUL", 3), q("o", 1, 0), ("QH", 3), ("RGV",) + SV[9], q("o", 1, 2), q(*SV[9])]
+    V += [("J5", 0, s) for s in range(4)] + [q("o", 2, 0), q("o", 2, 2)] + [("J5", 1, s) for s in range(4)]
+    V += [q("o", 3, 0), ("RGV",) + SV[10], q("o", 3, 2), q(*SV[10])] + [("J5", NB, s) for NB in (2, 3) for s in range(4)]
+    out, have = [], set()
+    streams = [D, A, PE, V]
+    while any(streams):
+        for s in streams:
+            n0 = len(out)
+            while s and all(x in have for x in needs(s[0])):
+                t = s.pop(0)
+                out.append(t)
+                have.add(t)
+                if t[0] in ("ldA", "ld"): have.add(t[:2] if t[0] == "ldA" else t[:4])
+                if t[0] in ("RGV", "RGS"): have.add(("RG",) + t[1:])
+                if s is V: break
+            if len(out) > n0: break
+        else:
+            assert False, [s[:1] for s in streams]
+    return out
 
 
 def tile_multiscaleretention_pb_kernel(tc, x, attn, Wg, bg, gn_w, gn_b, Wo, bo, out):
@@ -72,85 +109,78 @@ def tile_multiscaleretention_pb_kernel(tc, x, attn, Wg, bg, gn_w, gn_b, Wo, bo, 
         const = ctx.enter_context(tc.tile_pool(name="const", bufs=1))
         rawp = ctx.enter_context(tc.tile_pool(name="rawp", bufs=6))
         grpp = ctx.enter_context(tc.tile_pool(name="grpp", bufs=5))
-        codep = ctx.enter_context(tc.tile_pool(name="codep", bufs=6))
-        normp = ctx.enter_context(tc.tile_pool(name="normp", bufs=6))
+        grpv = ctx.enter_context(tc.tile_pool(name="grpv", bufs=3))
+        codep = ctx.enter_context(tc.tile_pool(name="codep", bufs=5))
+        normp = ctx.enter_context(tc.tile_pool(name="normp", bufs=8))
         gatep = ctx.enter_context(tc.tile_pool(name="gatep", bufs=2))
         outp = ctx.enter_context(tc.tile_pool(name="outp", bufs=6))
         psum = ctx.enter_context(tc.psum_pool(name="psum", bufs=8))
 
-
-        ident = const.tile([P, P], F32, name="ident")
-        make_identity(nc, ident[:])
-        vraw = const.tile([P, 512], BF16, name="vraw")
-        nc.vector.memset(vraw[:], 0.0)
+        warm = const.tile([P, 1], F32, name="warm")
+        nc.vector.memset(warm[:], 1.0)
         eps_t = const.tile([P, 1], F32, name="eps_t")
-        nc.vector.memset(eps_t[:], EPS)
+        nc.vector.tensor_scalar(out=eps_t[:], in0=warm[:], scalar1=EPS, scalar2=None, op0=ALU.mult)
+        vraw = const.tile([P, 512], BF16, name="vraw")
+        nc.gpsimd.memset(vraw[:], 0.0)
         nc.scalar.dma_start(out=vraw[0:4, :], in_=bg.rearrange("(r c) -> r c", c=512))
         nc.scalar.dma_start(out=vraw[4:8, :], in_=gn_w.rearrange("(r c) -> r c", c=512))
         nc.scalar.dma_start(out=vraw[8:12, :], in_=gn_b.rearrange("(r c) -> r c", c=512))
-        warm = const.tile([P, 1], F32, name="warm")
-        nc.scalar.activation(out=warm[:], in_=eps_t[:], func=ACT.Sqrt, scale=1.0)
-
-        bo_bc = const.tile([P, E], BF16, name="bo_bc")
-        vf = const.tile([P, 512], F32, name="vf")
-        vcol = const.tile([P, 4, 12], F32, name="vcol")
+        nc.scalar.activation(out=warm[:], in_=warm[:], func=ACT.Sqrt, scale=1.0)
+        ident = const.tile([P, P], F32, name="ident")
+        make_identity(nc, ident[:])
         st = const.tile([P, 64, 6], F32, name="st")
         dif = const.tile([P, 64], F32, name="dif")
         mu = const.tile([P, 64], F32, name="mu")
         m2 = const.tile([P, 64], F32, name="m2")
         std = const.tile([P, 64], F32, name="std")
         rstd = const.tile([P, 64], F32, name="rstd")
+
+        bo_bc = const.tile([P, E], BF16, name="bo_bc")
+        vf = const.tile([P, 512], F32, name="vf")
+        vcol = const.tile([P, 4, 12], F32, name="vcol")
         xc = const.tile([P, NPASS, S], U32, name="xc", align_bytes=64)
         xs = const.tile([P, NPASS, S], U8, name="xs", align_bytes=64)
         hc = const.tile([P, NPASS, S], U32, name="hc", align_bytes=64)
         hs = const.tile([P, NPASS, S], U8, name="hs", align_bytes=64)
         T = {}
 
-        def ld_attn(s):
-            T[("a", s)] = const.tile([P, E], BF16, name="a_sb%d" % s)
-            cuts = 2 if s == 0 else 1
+        def ld_attn(s, i=0, cuts=1):
+            if ("a", s) not in T:
+                T[("a", s)] = const.tile([P, E], BF16, name="a_sb%d" % s)
             w = E // cuts
-            for i in range(cuts):
-                nc.sync.dma_start(out=T[("a", s)][:, w * i:w * i + w], in_=af[P * s:P * s + P, w * i:w * i + w])
+            nc.sync.dma_start(out=T[("a", s)][:, w * i:w * i + w], in_=af[P * s:P * s + P, w * i:w * i + w])
 
-        def ld_raw(kind, a, c):
-            t = rawp.tile([P, 4096], BF16, name="raw_%s%d%d" % (kind, a, c), tag="raw")
-            T[("raw", kind, a, c)] = t
+        def ld_raw(kind, a, c, i=0, cuts=1):
+            if ("raw", kind, a, c) not in T:
+                T[("raw", kind, a, c)] = rawp.tile([P, 4096], BF16, name="raw_%s%d%d" % (kind, a, c), tag="raw")
+            t = T[("raw", kind, a, c)]
             if kind == "x":
                 nc.sync.dma_start(
                     out=t[:].rearrange("p (s k) -> p s k", s=2),
                     in_=xf[256 * a:256 * a + 256, :].rearrange("(s p) k -> p s k", p=P),
                 )
-            elif kind == "g":
-                tv = t[:].rearrange("p (t c) -> p t c", t=4)
-                cuts = 2 if (a == 0 and c == 0) else 1
-                w = 1024 // cuts
-                for i in range(cuts):
-                    c0 = 1024 * a + w * i
-                    nc.sync.dma_start(
-                        out=tv[:, :, w * i:w * i + w],
-                        in_=Wg[512 * c:512 * c + 512, c0:c0 + w].rearrange("(p j) c -> p j c", j=4),
-                    )
             else:
+                W = Wg if kind == "g" else Wo
+                tv = t[:].rearrange("p (j c) -> p j c", j=4)
+                w = 1024 // cuts
+                c0 = 1024 * a + w * i
                 nc.sync.dma_start(
-                    out=t[:].rearrange("p (t c) -> p t c", t=4),
-                    in_=Wo[512 * c:512 * c + 512, 1024 * a:1024 * a + 1024].rearrange("(p t) c -> p t c", t=4),
+                    out=tv[:, :, w * i:w * i + w],
+                    in_=W[512 * c:512 * c + 512, c0:c0 + w].rearrange("(p j) c -> p j c", j=4),
                 )
 
         def vec_prep():
-            nc.vector.tensor_copy(
+            nc.scalar.copy(
                 out=vf[:].rearrange("p (t m) -> p t m", t=4), in_=vraw[:].rearrange("p (m t) -> p t m", t=4)
             )
             vt = psum.tile([P, 4, P], F32, name="vt", tag="ps")
             for t in range(4):
                 nc.tensor.transpose(vt[:, t, :], vf[:, P * t:P * t + P], ident[:])
-            nc.vector.tensor_copy(out=vcol[:], in_=vt[:, :, 0:12])
+            nc.scalar.copy(out=vcol[:], in_=vt[:, :, 0:12])
 
         def bn(s):
             for g in range(16):
                 nc.vector.bn_stats(out=st[:, 16 * s + g, :], in_=T[("a", s)][:, P * g:P * g + P])
-            if s == 0:
-                vec_prep()
 
         def small():
             me, m2e, mo, m2o = st[:, :, 1], st[:, :, 2], st[:, :, 4], st[:, :, 5]
@@ -180,22 +210,29 @@ def tile_multiscaleretention_pb_kernel(tc, x, attn, Wg, bg, gn_w, gn_b, Wo, bo, 
                 out=xq32[:, 256 * sp:256 * sp + 256, :], in_=T[("xt", g, sp)][:].rearrange("p u r -> p r u")
             )
 
-        def regroup(eng, kind, blk, c):
+        def unit_views(eng, kind, blk, c):
             raw = T[("raw", kind, blk // 2, c)]
             col0 = 512 * (blk % 2)
-            src = raw[:].rearrange("p (t c) -> p t c", t=4)[:, :, col0:col0 + 512]
-            g4 = grpp.tile([P, 2048], BF16, name="g4_%s%d%d" % (kind, blk, c), tag="grp", align_bytes=64)
-            T[("g4", kind, blk, c)] = g4
+            src = raw[:].rearrange("p (j c) -> p j c", j=4)[:, :, col0:col0 + 512]
+            if ("g4", kind, blk, c) not in T:
+                pool = grpv if eng == "V" else grpp
+                T[("g4", kind, blk, c)] = pool.tile(
+                    [P, 2048], BF16, name="g4_%s%d%d" % (kind, blk, c), tag="grp", align_bytes=64
+                )
+            g4 = T[("g4", kind, blk, c)]
             if kind == "g":
-                dst = g4[:].rearrange("p (t m j) -> p m j t", t=4, j=4)
-                srcv = src.rearrange("p j (m t) -> p m j t", t=4)
-            else:
-                dst = g4[:].rearrange("p (c i t) -> p c t i", i=4, t=4)
-                srcv = src.rearrange("p t (c i) -> p c t i", i=4)
+                return (
+                    g4[:].rearrange("p (t m j) -> p m j t", t=4, j=4),
+                    src.rearrange("p j (m t) -> p m j t", t=4),
+                )
+            return g4[:].rearrange("p (c i j) -> p c j i", i=4, j=4), src.rearrange("p j (c i) -> p c j i", i=4)
+
+        def regroup(eng, kind, blk, c):
+            dst, src = unit_views(eng, kind, blk, c)
             if eng == "V":
-                nc.vector.tensor_copy(out=dst, in_=srcv)
+                nc.vector.tensor_copy(out=dst, in_=src)
             else:
-                nc.scalar.copy(out=dst, in_=srcv)
+                nc.scalar.copy(out=dst, in_=src)
 
         def quant(kind, blk, c):
             if ("wc", kind, blk) not in T:
@@ -229,11 +266,11 @@ def tile_multiscaleretention_pb_kernel(tc, x, attn, Wg, bg, gn_w, gn_b, Wo, bo, 
         def normalise(G, s):
             nrm = normp.tile([P, 512], F32, name="nrm%d%d" % (G, s), tag="nrm")
             T[("nrm", G, s)] = nrm
-            for t in range(4):
-                gi = 4 * G + t
+            for q in range(4):
+                gi = 4 * G + q
                 k = 16 * s + gi
                 nc.vector.tensor_scalar(
-                    out=nrm[:].rearrange("p (t m) -> p t m", t=4)[:, :, 32 * t:32 * t + 32],
+                    out=nrm[:].rearrange("p (t m) -> p t m", t=4)[:, :, 32 * q:32 * q + 32],
                     in0=T[("a", s)][:, P * gi:P * gi + P].rearrange("p (m t) -> p t m", t=4),
                     scalar1=mu[:, k:k + 1],
                     scalar2=rstd[:, k:k + 1],
@@ -264,7 +301,7 @@ def tile_multiscaleretention_pb_kernel(tc, x, attn, Wg, bg, gn_w, gn_b, Wo, bo, 
             )
 
         def gate_mul(G):
-            hq = grpp.tile([P, 2048], BF16, name="hq%d" % G, tag="grp", align_bytes=64)
+            hq = grpv.tile([P, 2048], BF16, name="hq%d" % G, tag="grp", align_bytes=64)
             T[("hq", G)] = hq
             nc.vector.tensor_tensor(
                 out=hq[:].rearrange("p (c i t) -> p c t i", i=4, t=4),
@@ -276,9 +313,7 @@ def tile_multiscaleretention_pb_kernel(tc, x, attn, Wg, bg, gn_w, gn_b, Wo, bo, 
         def mx2(NB, G):
             if G == 0:
                 for s in range(4):
-                    T[("acc", NB, s)] = psum.tile(
-                        [P, 512], F32, name="acc%d%d" % (NB, s), tag="ps"
-                    )
+                    T[("acc", NB, s)] = psum.tile([P, 512], F32, name="acc%d%d" % (NB, s), tag="ps")
             wc, ws = T[("wc", "o", NB)], T[("ws", "o", NB)]
             for s in range(4):
                 nc.tensor.matmul_mx(
@@ -298,16 +333,18 @@ def tile_multiscaleretention_pb_kernel(tc, x, attn, Wg, bg, gn_w, gn_b, Wo, bo, 
                 out=o_sb[:], in0=T[("acc", NB, s)][:], in1=bo_bc[:, 512 * NB:512 * NB + 512], op=ALU.add
             )
 
-        for tok in ORDER:
-            k = tok[0]
+        vec_prep()
+        ctx.enter_context(tc.manual_schedule())
+        for tok in pipeline():
+            k, arg = tok[0], tok[1:]
             if k == "ldA":
-                ld_attn(tok[1])
+                ld_attn(*arg)
             elif k == "ld":
-                ld_raw(tok[1], tok[2], tok[3])
+                ld_raw(*arg)
             elif k == "ldbo":
                 nc.sync.dma_start(out=bo_bc[:], in_=bo.partition_broadcast(P))
             elif k == "bn":
-                bn(tok[1])
+                bn(*arg)
             elif k == "sm":
                 small()
             elif k == "sqrt":
@@ -315,41 +352,51 @@ def tile_multiscaleretention_pb_kernel(tc, x, attn, Wg, bg, gn_w, gn_b, Wo, bo, 
             elif k == "recip":
                 nc.vector.reciprocal(out=rstd[:], in_=std[:])
             elif k == "xT":
-                x_transpose(tok[1], tok[2])
+                x_transpose(*arg)
             elif k == "XE":
-                x_evac(tok[1], tok[2])
+                x_evac(*arg)
             elif k == "Qx":
                 nc.vector.quantize_mx(
-                    out=xc[:, tok[1], :].bitcast(FP8X4), scales=xs[:, tok[1], :], in_=T[("xq", tok[1])][:]
+                    out=xc[:, arg[0], :].bitcast(FP8X4), scales=xs[:, arg[0], :], in_=T[("xq", arg[0])][:]
                 )
             elif k == "RGV":
-                regroup("V", tok[1], tok[2], tok[3])
+                regroup("V", *arg)
             elif k == "RGS":
-                regroup("S", tok[1], tok[2], tok[3])
+                regroup("S", *arg)
             elif k == "Q":
-                quant(tok[1], tok[2], tok[3])
+                quant(*arg)
             elif k == "MX1":
-                mx1(tok[1], tok[2])
+                mx1(*arg)
             elif k == "J4":
-                normalise(tok[1], tok[2])
+                normalise(*arg)
             elif k == "T":
-                n_transpose(tok[1], tok[2])
+                n_transpose(*arg)
             elif k == "SIL":
-                silu(tok[1], tok[2])
+                silu(*arg)
             elif k == "GW":
-                gain(tok[1], tok[2])
+                gain(*arg)
             elif k == "MUL":
-                gate_mul(tok[1])
+                gate_mul(*arg)
             elif k == "QH":
                 nc.vector.quantize_mx(
-                    out=hc[:, tok[1], :].bitcast(FP8X4), scales=hs[:, tok[1], :], in_=T[("hq", tok[1])][:]
+                    out=hc[:, arg[0], :].bitcast(FP8X4), scales=hs[:, arg[0], :], in_=T[("hq", arg[0])][:]
                 )
             elif k == "MX2":
-                mx2(tok[1], tok[2])
+                mx2(*arg)
             elif k == "J5":
-                bias_out(tok[1], tok[2])
+                bias_out(*arg)
+            elif k == "E5a":
+                NB, s = arg
+                T[("o", NB, s)] = outp.tile([P, 512], F32, name="o%d%d" % (NB, s), tag="o")
+                nc.scalar.copy(out=T[("o", NB, s)][:], in_=T[("acc", NB, s)][:])
+            elif k == "E5b":
+                NB, s = arg
+                o_sb = T[("o", NB, s)]
+                nc.gpsimd.tensor_tensor(
+                    out=o_sb[:], in0=o_sb[:], in1=bo_bc[:, 512 * NB:512 * NB + 512], op=ALU.add
+                )
             elif k == "st":
-                NB, s = tok[1], tok[2]
+                NB, s = arg
                 nc.sync.dma_start(out=of[P * s:P * s + P, 512 * NB:512 * NB + 512], in_=T[("o", NB, s)][:])
             else:
                 assert False, k

@@ -26,15 +26,14 @@ CV = (2, 3, 2, 2)
 def needs(t):
     k = t[0]
     if k == "bn": return [("ldA", t[1])]
-    if k == "sm": return [("bn", s) for s in range(4)]
-    if k == "sqrt": return [("sm",)]
-    if k == "recip": return [("sqrt",)]
+    if k == "sqrt": return [("bn", t[1])]
+    if k == "recip": return [("sqrt", t[1])]
     if k == "xT": return [("ld", "x", t[2], 0)]
     if k == "XE": return [("xT",) + t[1:]]
     if k == "Qx": return [("XE", t[1], 0), ("XE", t[1], 1)]
     if k in ("RGV", "RGS"): return [("ld", t[1], t[2] // 2, t[3])]
     if k == "Q": return [("RG",) + t[1:]]
-    if k == "J4": return [("recip",)]
+    if k == "J4": return [("recip", t[2])]
     if k == "T": return [("J4", t[1], s) for s in range(4)]
     if k == "GW": return [("T",) + t[1:]]
     if k == "MX1": return [("Q", "g", t[1], c) for c in range(4)] + [("Qx", c) for c in range(4)]
@@ -56,8 +55,8 @@ def pipeline():
     D += [("ld", "g", 1, c) for c in range(4)] + [("ldbo",)]
     D += [("ld", "o", a, c) for a in range(2) for c in range(4)]
     D += [("st", NB, s) for NB in range(4) for s in range(4)]
-    A += [("RGS", "g", 0, 0), ("RGS", "g", 0, 1), ("RGS", "g", 1, 1), ("RGS", "g", 0, 2), ("RGS", "g", 0, 3)]
-    A += [("XE", g, 0) for g in range(4)] + [("XE", 0, 1), ("XE", 1, 1), ("sqrt",), ("XE", 2, 1), ("XE", 3, 1)]
+    A += [("RGS", "g", 0, 0), ("sqrt", 0), ("RGS", "g", 0, 1), ("RGS", "g", 1, 1), ("sqrt", 1), ("RGS", "g", 0, 2), ("sqrt", 2), ("RGS", "g", 0, 3), ("sqrt", 3)]
+    A += [("XE", g, 0) for g in range(4)] + [("XE", g, 1) for g in range(4)]
     sa = list(SA)
     for G in range(4):
         for i in range(CA[G]): A.append(("RGS",) + sa.pop(0))
@@ -70,9 +69,8 @@ def pipeline():
         if G < 3: PE += [("T", G + 1, t) for t in range(4)]
     PE += [("MX2", NB, G) for NB in range(4) for G in range(4)]
     q = lambda kind, b, c: ("Q", kind, b, c)
-    V += [("bn", 0), ("RGV", "g", 1, 0), ("bn", 1), q("g", 0, 0), q("g", 1, 0), ("bn", 2), q("g", 0, 1), q("g", 1, 1), ("RGV", "g", 1, 2)]
-    V += [("bn", 3), q("g", 0, 2), q("g", 1, 2), ("RGV", "g", 1, 3), ("sm",), q("g", 0, 3), q("g", 1, 3), ("Qx", 0), ("recip",), ("Qx", 1), ("Qx", 2), ("Qx", 3)]
-    V += [("J4", 0, s) for s in range(4)]
+    V += [("bn", 0), ("RGV", "g", 1, 0), ("bn", 1), q("g", 0, 0), q("g", 1, 0), ("bn", 2), ("recip", 0), ("J4", 0, 0), q("g", 0, 1), ("recip", 1), ("J4", 0, 1), ("RGV", "g", 1, 2), q("g", 1, 1)]
+    V += [("bn", 3), ("recip", 2), q("g", 0, 2), q("g", 1, 2), ("RGV", "g", 1, 3), ("recip", 3), q("g", 0, 3), q("g", 1, 3), ("J4", 0, 2), ("J4", 0, 3), ("Qx", 0), ("Qx", 1), ("Qx", 2), ("Qx", 3)]
     V += [q("g", 2, 0), ("RGV",) + SV[0], ("J4", 1, 0), q("g", 2, 1), ("J4", 1, 1), ("J4", 1, 2), ("J4", 1, 3), q("g", 3, 0), ("RGV",) + SV[1], ("J4", 2, 0), q("g", 3, 1)]
     V += [("J4", 2, s) for s in range(1, 4)]
     V += [("MUL", 0), q("g", 2, 2), ("QH", 0), ("RGV",) + SV[2], q("g", 2, 3), q(*SV[2]), ("RGV",) + SV[3], ("RGV",) + SV[4], q(*SV[3]), q(*SV[4])]
@@ -128,12 +126,8 @@ def tile_multiscaleretention_pb_kernel(tc, x, attn, Wg, bg, gn_w, gn_b, Wo, bo, 
         nc.scalar.activation(out=warm[:], in_=warm[:], func=ACT.Sqrt, scale=1.0)
         ident = const.tile([P, P], F32, name="ident")
         make_identity(nc, ident[:])
-        st = const.tile([P, 64, 6], F32, name="st")
-        dif = const.tile([P, 64], F32, name="dif")
-        mu = const.tile([P, 64], F32, name="mu")
-        m2 = const.tile([P, 64], F32, name="m2")
-        std = const.tile([P, 64], F32, name="std")
-        rstd = const.tile([P, 64], F32, name="rstd")
+        identb = const.tile([P, P], BF16, name="identb")
+        make_identity(nc, identb[:])
 
         bo_bc = const.tile([P, E], BF16, name="bo_bc")
         vf = const.tile([P, 512], F32, name="vf")
@@ -179,19 +173,22 @@ def tile_multiscaleretention_pb_kernel(tc, x, attn, Wg, bg, gn_w, gn_b, Wo, bo, 
             nc.scalar.copy(out=vcol[:], in_=vt[:, :, 0:12])
 
         def bn(s):
-            for g in range(16):
-                nc.vector.bn_stats(out=st[:, 16 * s + g, :], in_=T[("a", s)][:, P * g:P * g + P])
+            st = const.tile([P, 8, 6], F32, name="st%d" % s)
+            T[("st", s)] = st
+            for i in range(8):
+                nc.vector.bn_stats(
+                    out=st[:, i, :], in_=T[("a", s)][:, 256 * i:256 * i + 256].rearrange("p (g c) -> p c g", g=2)
+                )
 
-        def small():
-            me, m2e, mo, m2o = st[:, :, 1], st[:, :, 2], st[:, :, 4], st[:, :, 5]
-            nc.vector.tensor_tensor(out=dif[:], in0=me, in1=mo, op=ALU.subtract)
-            nc.vector.tensor_tensor(out=mu[:], in0=me, in1=mo, op=ALU.add)
-            nc.vector.tensor_tensor(out=m2[:], in0=m2e, in1=m2o, op=ALU.add)
-            nc.vector.tensor_tensor(out=dif[:], in0=dif[:], in1=dif[:], op=ALU.mult)
-            nc.vector.tensor_scalar(out=mu[:], in0=mu[:], scalar1=0.5, scalar2=None, op0=ALU.mult)
-            nc.vector.scalar_tensor_tensor(
-                out=m2[:], in0=dif[:], scalar=32.0, in1=m2[:], op0=ALU.mult, op1=ALU.add
+        def root(s):
+            T[("std", s)] = const.tile([P, 8, 2], F32, name="std%d" % s)
+            nc.scalar.activation(
+                out=T[("std", s)][:], in_=T[("st", s)][:, :, 2:6:3], func=ACT.Sqrt, bias=eps_t[:, 0:1], scale=1.0 / P
             )
+
+        def recip(s):
+            T[("rstd", s)] = const.tile([P, 8, 2], F32, name="rstd%d" % s)
+            nc.vector.reciprocal(out=T[("rstd", s)][:], in_=T[("std", s)][:])
 
         def x_transpose(g, sp):
             xt = psum.tile([P, 2, 256], F32, name="xt%d%d" % (g, sp), tag="ps")
@@ -234,6 +231,34 @@ def tile_multiscaleretention_pb_kernel(tc, x, attn, Wg, bg, gn_w, gn_b, Wo, bo, 
             else:
                 nc.scalar.copy(out=dst, in_=src)
 
+        def tensor_pass(kind, blk, c):
+            raw = T[("raw", kind, blk // 2, c)]
+            src = raw[:].rearrange("p (j c) -> p j c", j=4)[:, :, 512 * (blk % 2):512 * (blk % 2) + 512]
+            for h in range(2):
+                pt = psum.tile([P, 1024], BF16, name="pt_%s%d%d%d" % (kind, blk, c, h), tag="ps")
+                T[("pt", kind, blk, c, h)] = pt
+                for j in range(4):
+                    mov = src[:, j, 256 * h:256 * h + 256]
+                    if kind == "g":
+                        dst = pt[:].rearrange("p (t m j) -> p j m t", t=4, j=4)[:, j]
+                        mov = mov.rearrange("p (m t) -> p m t", t=4)
+                    else:
+                        dst = pt[:].rearrange("p (c j) -> p j c", j=4)[:, j]
+                    nc.tensor.matmul(dst, lhsT=identb[:], rhs=mov, start=True, stop=True)
+
+        def tensor_pass_out(kind, blk, c):
+            g4 = grpp.tile([P, 2048], BF16, name="g4_%s%d%d" % (kind, blk, c), tag="grp", align_bytes=64)
+            T[("g4", kind, blk, c)] = g4
+            for h in range(2):
+                pt = T[("pt", kind, blk, c, h)]
+                if kind == "g":
+                    nc.scalar.copy(
+                        out=g4[:].rearrange("p (t r) -> p t r", t=4)[:, :, 256 * h:256 * h + 256],
+                        in_=pt[:].rearrange("p (t r) -> p t r", t=4),
+                    )
+                else:
+                    nc.scalar.copy(out=g4[:, 1024 * h:1024 * h + 1024], in_=pt[:])
+
         def quant(kind, blk, c):
             if ("wc", kind, blk) not in T:
                 T[("wc", kind, blk)] = codep.tile(
@@ -268,12 +293,12 @@ def tile_multiscaleretention_pb_kernel(tc, x, attn, Wg, bg, gn_w, gn_b, Wo, bo, 
             T[("nrm", G, s)] = nrm
             for q in range(4):
                 gi = 4 * G + q
-                k = 16 * s + gi
+                i, e = gi // 2, gi % 2
                 nc.vector.tensor_scalar(
                     out=nrm[:].rearrange("p (t m) -> p t m", t=4)[:, :, 32 * q:32 * q + 32],
                     in0=T[("a", s)][:, P * gi:P * gi + P].rearrange("p (m t) -> p t m", t=4),
-                    scalar1=mu[:, k:k + 1],
-                    scalar2=rstd[:, k:k + 1],
+                    scalar1=T[("st", s)][:, i, 1 + 3 * e:2 + 3 * e],
+                    scalar2=T[("rstd", s)][:, i, e:e + 1],
                     op0=ALU.subtract,
                     op1=ALU.mult,
                 )
@@ -334,7 +359,6 @@ def tile_multiscaleretention_pb_kernel(tc, x, attn, Wg, bg, gn_w, gn_b, Wo, bo, 
             )
 
         vec_prep()
-        ctx.enter_context(tc.manual_schedule())
         for tok in pipeline():
             k, arg = tok[0], tok[1:]
             if k == "ldA":
@@ -345,12 +369,14 @@ def tile_multiscaleretention_pb_kernel(tc, x, attn, Wg, bg, gn_w, gn_b, Wo, bo, 
                 nc.sync.dma_start(out=bo_bc[:], in_=bo.partition_broadcast(P))
             elif k == "bn":
                 bn(*arg)
-            elif k == "sm":
-                small()
             elif k == "sqrt":
-                nc.scalar.activation(out=std[:], in_=m2[:], func=ACT.Sqrt, bias=eps_t[:, 0:1], scale=1.0 / P)
+                root(*arg)
             elif k == "recip":
-                nc.vector.reciprocal(out=rstd[:], in_=std[:])
+                recip(*arg)
+            elif k == "PI":
+                tensor_pass(*arg)
+            elif k == "PE":
+                tensor_pass_out(*arg)
             elif k == "xT":
                 x_transpose(*arg)
             elif k == "XE":

@@ -18,8 +18,8 @@ EPS = 1e-5
 NPASS = E // 512
 FLOPS = 2 * 2 * S * E * E
 
-SA = [("g", 2, 0), ("g", 3, 0), ("g", 2, 2), ("g", 2, 3), ("g", 3, 2), ("g", 3, 3), ("o", 0, 1), ("o", 1, 0), ("o", 1, 2), ("o", 2, 0), ("o", 2, 2), ("o", 3, 0), ("o", 3, 2)]
-SV = [("g", 2, 1), ("g", 3, 1), ("o", 0, 0), ("o", 0, 2), ("o", 0, 3), ("o", 1, 1), ("o", 1, 3), ("o", 2, 1), ("o", 3, 1), ("o", 2, 3), ("o", 3, 3)]
+SA = [("g", 2, 0), ("g", 3, 0), ("g", 2, 2), ("g", 2, 3), ("g", 3, 2), ("g", 3, 3), ("o", 0, 1), ("o", 2, 0), ("o", 2, 2), ("o", 2, 3), ("o", 3, 0), ("o", 3, 2), ("o", 3, 3)]
+SV = [("g", 2, 1), ("g", 3, 1), ("o", 0, 0), ("o", 0, 2), ("o", 0, 3), ("o", 1, 0), ("o", 1, 1), ("o", 1, 2), ("o", 1, 3), ("o", 2, 1), ("o", 3, 1)]
 CA = (2, 2, 2, 1)
 CV = (2, 3, 2, 2)
 
@@ -67,7 +67,8 @@ def pipeline():
     for G in range(4):
         PE += [("MX1", G, t) for t in range(4)]
         if G < 3: PE += [("T", G + 1, t) for t in range(4)]
-    PE += [("MX2", NB, G) for NB in range(4) for G in range(4)]
+    PE += [("MX2", NB, G) for NB in range(2) for G in range(3)] + [("MX2", NB, 3) for NB in range(2)]
+    PE += [("MX2", NB, G) for NB in (2, 3) for G in range(4)]
     q = lambda kind, b, c: ("Q", kind, b, c)
     V += [("bn", 0), ("RGV", "g", 1, 0), ("bn", 1), q("g", 0, 0), q("g", 1, 0), ("bn", 2), ("recip", 0), ("J4", 0, 0), q("g", 0, 1), ("recip", 1), ("J4", 0, 1), ("RGV", "g", 1, 2), q("g", 1, 1)]
     V += [("bn", 3), ("recip", 2), q("g", 0, 2), q("g", 1, 2), ("RGV", "g", 1, 3), ("recip", 3), q("g", 0, 3), q("g", 1, 3), ("J4", 0, 2), ("J4", 0, 3), ("Qx", 0), ("Qx", 1), ("Qx", 2), ("Qx", 3)]
@@ -76,9 +77,8 @@ def pipeline():
     V += [("MUL", 0), q("g", 2, 2), ("QH", 0), ("RGV",) + SV[2], q("g", 2, 3), q(*SV[2]), ("RGV",) + SV[3], ("RGV",) + SV[4], q(*SV[3]), q(*SV[4])]
     V += [("MUL", 1), q("g", 3, 2), ("QH", 1)] + [("J4", 3, s) for s in range(2)] + [q("g", 3, 3)] + [("J4", 3, s) for s in range(2, 4)]
     V += [("RGV",) + SV[5], ("RGV",) + SV[6], q(*SV[5]), q(*SV[6]), ("MUL", 2), q("o", 0, 1), ("QH", 2), ("RGV",) + SV[7], ("RGV",) + SV[8], q(*SV[7]), q(*SV[8])]
-    V += [("MUL", 3), q("o", 1, 0), ("QH", 3), ("RGV",) + SV[9], q("o", 1, 2), q(*SV[9])]
-    V += [("J5", 0, s) for s in range(4)] + [q("o", 2, 0), q("o", 2, 2)] + [("J5", 1, s) for s in range(4)]
-    V += [q("o", 3, 0), ("RGV",) + SV[10], q("o", 3, 2), q(*SV[10])] + [("J5", NB, s) for NB in (2, 3) for s in range(4)]
+    V += [("MUL", 3), ("RGV",) + SV[9], ("QH", 3), q("o", 2, 0), q(*SV[9]), q("o", 2, 2)]
+    V += [("J5", 0, s) for s in range(0, 4)] + [q("o", 2, 3), ("RGV",) + SV[10], q("o", 3, 0)] + [("J5", 1, s) for s in range(0, 4)] + [q(*SV[10]), q("o", 3, 2)] + [("J5", 2, s) for s in range(0, 2)] + [q("o", 3, 3)] + [("J5", 2, s) for s in range(2, 4)] + [("J5", 3, s) for s in range(0, 4)]
     out, have = [], set()
     streams = [D, A, PE, V]
     while any(streams):

@@ -18,9 +18,9 @@ EPS = 1e-5
 NPASS = E // 512
 FLOPS = 2 * 2 * S * E * E
 
-SA = [("g", 2, 0), ("g", 3, 0), ("g", 2, 2), ("g", 2, 3), ("g", 3, 2), ("g", 3, 3), ("o", 0, 1), ("o", 2, 0), ("o", 2, 2), ("o", 2, 3), ("o", 3, 0), ("o", 3, 2), ("o", 3, 3)]
+SA = [("g", 2, 0), ("g", 3, 0), ("g", 2, 2), ("g", 3, 2), ("o", 0, 1), ("o", 2, 0), ("o", 2, 2), ("o", 2, 3), ("o", 3, 0), ("o", 3, 2), ("o", 3, 3)]
 SV = [("g", 2, 1), ("g", 3, 1), ("o", 0, 0), ("o", 0, 2), ("o", 0, 3), ("o", 1, 0), ("o", 1, 1), ("o", 1, 2), ("o", 1, 3), ("o", 2, 1), ("o", 3, 1)]
-CA = (2, 2, 2, 1)
+CA = (2, 1, 1, 1)
 CV = (2, 3, 2, 2)
 
 def needs(t):
@@ -72,12 +72,12 @@ def pipeline():
     q = lambda kind, b, c: ("Q", kind, b, c)
     V += [("bn", 0), ("RGV", "g", 1, 0), ("bn", 1), q("g", 0, 0), q("g", 1, 0), ("bn", 2), ("recip", 0), ("J4", 0, 0), q("g", 0, 1), ("recip", 1), ("J4", 0, 1), ("RGV", "g", 1, 2), q("g", 1, 1)]
     V += [("bn", 3), ("recip", 2), q("g", 0, 2), q("g", 1, 2), ("RGV", "g", 1, 3), ("recip", 3), q("g", 0, 3), q("g", 1, 3), ("J4", 0, 2), ("J4", 0, 3), ("Qx", 0), ("Qx", 1), ("Qx", 2), ("Qx", 3)]
-    V += [q("g", 2, 0), ("RGV",) + SV[0], ("J4", 1, 0), q("g", 2, 1), ("J4", 1, 1), ("J4", 1, 2), ("J4", 1, 3), q("g", 3, 0), ("RGV",) + SV[1], ("J4", 2, 0), q("g", 3, 1)]
+    V += [q("g", 2, 0), ("RGV",) + SV[0], ("J4", 1, 0), q("g", 2, 1), ("J4", 1, 1), ("J4", 1, 2), ("J4", 1, 3), ("RGV", "g", 2, 3), q("g", 3, 0), ("RGV",) + SV[1], ("J4", 2, 0), q("g", 3, 1)]
     V += [("J4", 2, s) for s in range(1, 4)]
     V += [("MUL", 0), q("g", 2, 2), ("QH", 0), ("RGV",) + SV[2], q("g", 2, 3), q(*SV[2]), ("RGV",) + SV[3], ("RGV",) + SV[4], q(*SV[3]), q(*SV[4])]
-    V += [("MUL", 1), q("g", 3, 2), ("QH", 1)] + [("J4", 3, s) for s in range(2)] + [q("g", 3, 3)] + [("J4", 3, s) for s in range(2, 4)]
-    V += [("RGV",) + SV[5], ("RGV",) + SV[6], q(*SV[5]), q(*SV[6]), ("MUL", 2), q("o", 0, 1), ("QH", 2), ("RGV",) + SV[7], ("RGV",) + SV[8], q(*SV[7]), q(*SV[8])]
-    V += [("MUL", 3), ("RGV",) + SV[9], ("QH", 3), q("o", 2, 0), q(*SV[9]), q("o", 2, 2)]
+    V += [("MUL", 1), ("RGV", "g", 3, 3), q("g", 3, 2), ("QH", 1)] + [("J4", 3, s) for s in range(2)] + [q("g", 3, 3)] + [("J4", 3, s) for s in range(2, 4)]
+    V += [("RGV",) + SV[5], ("MUL", 2), q("o", 0, 1), ("QH", 2), ("RGV",) + SV[6], q(*SV[5]), q(*SV[6])]
+    V += [("MUL", 3), ("RGV",) + SV[7], ("QH", 3), ("RGV",) + SV[8], q(*SV[7]), q(*SV[8]), ("RGV",) + SV[9], q("o", 2, 0), q(*SV[9]), q("o", 2, 2)]
     V += [("J5", 0, s) for s in range(0, 4)] + [q("o", 2, 3), ("RGV",) + SV[10], q("o", 3, 0)] + [("J5", 1, s) for s in range(0, 4)] + [q(*SV[10]), q("o", 3, 2)] + [("J5", 2, s) for s in range(0, 2)] + [q("o", 3, 3)] + [("J5", 2, s) for s in range(2, 4)] + [("J5", 3, s) for s in range(0, 4)]
     out, have = [], set()
     streams = [D, A, PE, V]
@@ -202,9 +202,10 @@ def tile_multiscaleretention_pb_kernel(tc, x, attn, Wg, bg, gn_w, gn_b, Wo, bo, 
         def x_evac(g, sp):
             if ("xq", g) not in T:
                 T[("xq", g)] = grpp.tile([P, 2048], BF16, name="xq%d" % g, tag="grp", align_bytes=64)
-            xq32 = T[("xq", g)][:].bitcast(F32).rearrange("p (r u) -> p r u", u=2)
+            xq32 = T[("xq", g)][:].bitcast(F32)[:, 512 * sp:512 * sp + 512]
             nc.scalar.copy(
-                out=xq32[:, 256 * sp:256 * sp + 256, :], in_=T[("xt", g, sp)][:].rearrange("p u r -> p r u")
+                out=xq32.rearrange("p (r i u) -> p r u i", i=2, u=2),
+                in_=T[("xt", g, sp)][:].rearrange("p u (r i) -> p r u i", i=2),
             )
 
         def unit_views(eng, kind, blk, c):

from contextlib import ExitStack

import concourse.mybir as mybir
from concourse.masks import make_identity

F32 = mybir.dt.float32
BF16 = mybir.dt.bfloat16
U32 = mybir.dt.uint32
U8 = mybir.dt.uint8
FP8X4 = mybir.dt.float8_e4m3fn_x4
ALU = mybir.AluOpType
ACT = mybir.ActivationFunctionType

P = 128
S = 512
E = 2048
EPS = 1e-5
NPASS = E // 512
FLOPS = 2 * 2 * S * E * E

SA = [("g", 2, 0), ("g", 3, 0), ("g", 2, 2), ("g", 3, 2), ("o", 0, 1), ("o", 2, 0), ("o", 2, 2), ("o", 2, 3), ("o", 3, 0), ("o", 3, 2), ("o", 3, 3)]
SV = [("g", 2, 1), ("g", 3, 1), ("o", 0, 0), ("o", 0, 2), ("o", 0, 3), ("o", 1, 0), ("o", 1, 1), ("o", 1, 2), ("o", 1, 3), ("o", 2, 1), ("o", 3, 1)]
CA = (2, 1, 1, 1)
CV = (2, 3, 2, 2)

def needs(t):
    k = t[0]
    if k == "bn": return [("ldA", t[1])]
    if k == "sqrt": return [("bn", t[1])]
    if k == "recip": return [("sqrt", t[1])]
    if k == "xT": return [("ld", "x", t[2], 0)]
    if k == "XE": return [("xT",) + t[1:]]
    if k == "Qx": return [("XE", t[1], 0), ("XE", t[1], 1)]
    if k in ("RGV", "RGS"): return [("ld", t[1], t[2] // 2, t[3])]
    if k == "Q": return [("RG",) + t[1:]]
    if k == "J4": return [("recip", t[2])]
    if k == "T": return [("J4", t[1], s) for s in range(4)]
    if k == "GW": return [("T",) + t[1:]]
    if k == "MX1": return [("Q", "g", t[1], c) for c in range(4)] + [("Qx", c) for c in range(4)]
    if k == "SIL": return [("MX1",) + t[1:]]
    if k == "MUL": return [("SIL", t[1], 3), ("GW", t[1], 3)]
    if k == "QH": return [("MUL", t[1])]
    if k == "MX2": return [("QH", t[2]), ("Q", "o", t[1], t[2])]
    if k == "J5": return [("MX2", t[1], 3), ("ldbo",)]
    if k == "st": return [("J5",) + t[1:]]
    return []

def pipeline():
    D, V, A, PE = [], [], [], []
    for i in range(2):
        D += [("ldA", 0, 2 * i, 4), ("ldA", 0, 2 * i + 1, 4), ("ld", "g", 0, 0, i, 2)]
    for c in range(1, 4):
        D += [("ldA", c), ("ld", "g", 0, c)]
    D += [("ld", "x", sp, 0) for sp in range(2)]
    D += [("ld", "g", 1, c) for c in range(4)] + [("ldbo",)]
    D += [("ld", "o", a, c) for a in range(2) for c in range(4)]
    D += [("st", NB, s) for NB in range(4) for s in range(4)]
    A += [("RGS", "g", 0, 0), ("sqrt", 0), ("RGS", "g", 0, 1), ("RGS", "g", 1, 1), ("sqrt", 1), ("RGS", "g", 0, 2), ("sqrt", 2), ("RGS", "g", 0, 3), ("sqrt", 3)]
    A += [("XE", g, 0) for g in range(4)] + [("XE", g, 1) for g in range(4)]
    sa = list(SA)
    for G in range(4):
        for i in range(CA[G]): A.append(("RGS",) + sa.pop(0))
        A += [("GW", G, t) for t in range(4)] + [("SIL", G, t) for t in range(4)]
    A += [("RGS",) + u for u in sa]
    PE += [("xT", g, sp) for sp in range(2) for g in range(4)]
    PE += [("T", 0, t) for t in range(4)]
    for G in range(4):
        PE += [("MX1", G, t) for t in range(4)]
        if G < 3: PE += [("T", G + 1, t) for t in range(4)]
    PE += [("MX2", NB, G) for NB in range(2) for G in range(3)] + [("MX2", NB, 3) for NB in range(2)]
    PE += [("MX2", NB, G) for NB in (2, 3) for G in range(4)]
    q = lambda kind, b, c: ("Q", kind, b, c)
    V += [("bn", 0), ("RGV", "g", 1, 0), ("bn", 1), q("g", 0, 0), q("g", 1, 0), ("bn", 2), ("recip", 0), ("J4", 0, 0), q("g", 0, 1), ("recip", 1), ("J4", 0, 1), ("RGV", "g", 1, 2), q("g", 1, 1)]
    V += [("bn", 3), ("recip", 2), q("g", 0, 2), q("g", 1, 2), ("RGV", "g", 1, 3), ("recip", 3), q("g", 0, 3), q("g", 1, 3), ("J4", 0, 2), ("J4", 0, 3), ("Qx", 0), ("Qx", 1), ("Qx", 2), ("Qx", 3)]
    V += [q("g", 2, 0), ("RGV",) + SV[0], ("J4", 1, 0), q("g", 2, 1), ("J4", 1, 1), ("J4", 1, 2), ("J4", 1, 3), ("RGV", "g", 2, 3), q("g", 3, 0), ("RGV",) + SV[1], ("J4", 2, 0), q("g", 3, 1)]
    V += [("J4", 2, s) for s in range(1, 4)]
    V += [("MUL", 0), q("g", 2, 2), ("QH", 0), ("RGV",) + SV[2], q("g", 2, 3), q(*SV[2]), ("RGV",) + SV[3], ("RGV",) + SV[4], q(*SV[3]), q(*SV[4])]
    V += [("MUL", 1), ("RGV", "g", 3, 3), q("g", 3, 2), ("QH", 1)] + [("J4", 3, s) for s in range(2)] + [q("g", 3, 3)] + [("J4", 3, s) for s in range(2, 4)]
    V += [("RGV",) + SV[5], ("MUL", 2), q("o", 0, 1), ("QH", 2), ("RGV",) + SV[6], q(*SV[5]), q(*SV[6])]
    V += [("MUL", 3), ("RGV",) + SV[7], ("QH", 3), ("RGV",) + SV[8], q(*SV[7]), q(*SV[8]), ("RGV",) + SV[9], q("o", 2, 0), q(*SV[9]), q("o", 2, 2)]
    V += [("J5", 0, s) for s in range(0, 4)] + [q("o", 2, 3), ("RGV",) + SV[10], q("o", 3, 0)] + [("J5", 1, s) for s in range(0, 4)] + [q(*SV[10]), q("o", 3, 2)] + [("J5", 2, s) for s in range(0, 2)] + [q("o", 3, 3)] + [("J5", 2, s) for s in range(2, 4)] + [("J5", 3, s) for s in range(0, 4)]
    out, have = [], set()
    streams = [D, A, PE, V]
    while any(streams):
        for s in streams:
            n0 = len(out)
            while s and all(x in have for x in needs(s[0])):
                t = s.pop(0)
                out.append(t)
                have.add(t)
                if t[0] in ("ldA", "ld"): have.add(t[:2] if t[0] == "ldA" else t[:4])
                if t[0] in ("RGV", "RGS"): have.add(("RG",) + t[1:])
                if s is V: break
            if len(out) > n0: break
        else:
            assert False, [s[:1] for s in streams]
    return out


def tile_multiscaleretention_pb_kernel(tc, x, attn, Wg, bg, gn_w, gn_b, Wo, bo, out):
    nc = tc.nc
    xf = x.flatten_outer_dims()
    af = attn.flatten_outer_dims()
    of = out.flatten_outer_dims()

    with ExitStack() as ctx:
        const = ctx.enter_context(tc.tile_pool(name="const", bufs=1))
        rawp = ctx.enter_context(tc.tile_pool(name="rawp", bufs=6))
        grpp = ctx.enter_context(tc.tile_pool(name="grpp", bufs=5))
        grpv = ctx.enter_context(tc.tile_pool(name="grpv", bufs=3))
        codep = ctx.enter_context(tc.tile_pool(name="codep", bufs=5))
        normp = ctx.enter_context(tc.tile_pool(name="normp", bufs=8))
        gatep = ctx.enter_context(tc.tile_pool(name="gatep", bufs=2))
        outp = ctx.enter_context(tc.tile_pool(name="outp", bufs=6))
        psum = ctx.enter_context(tc.psum_pool(name="psum", bufs=8))

        warm = const.tile([P, 1], F32, name="warm")
        nc.vector.memset(warm[:], 1.0)
        eps_t = const.tile([P, 1], F32, name="eps_t")
        nc.vector.tensor_scalar(out=eps_t[:], in0=warm[:], scalar1=EPS, scalar2=None, op0=ALU.mult)
        vraw = const.tile([P, 512], BF16, name="vraw")
        nc.gpsimd.memset(vraw[:], 0.0)
        nc.scalar.dma_start(out=vraw[0:4, :], in_=bg.rearrange("(r c) -> r c", c=512))
        nc.scalar.dma_start(out=vraw[4:8, :], in_=gn_w.rearrange("(r c) -> r c", c=512))
        nc.scalar.dma_start(out=vraw[8:12, :], in_=gn_b.rearrange("(r c) -> r c", c=512))
        nc.scalar.activation(out=warm[:], in_=warm[:], func=ACT.Sqrt, scale=1.0)
        ident = const.tile([P, P], F32, name="ident")
        make_identity(nc, ident[:])
        identb = const.tile([P, P], BF16, name="identb")
        make_identity(nc, identb[:])

        bo_bc = const.tile([P, E], BF16, name="bo_bc")
        vf = const.tile([P, 512], F32, name="vf")
        vcol = const.tile([P, 4, 12], F32, name="vcol")
        xc = const.tile([P, NPASS, S], U32, name="xc", align_bytes=64)
        xs = const.tile([P, NPASS, S], U8, name="xs", align_bytes=64)
        hc = const.tile([P, NPASS, S], U32, name="hc", align_bytes=64)
        hs = const.tile([P, NPASS, S], U8, name="hs", align_bytes=64)
        T = {}

        def ld_attn(s, i=0, cuts=1):
            if ("a", s) not in T:
                T[("a", s)] = const.tile([P, E], BF16, name="a_sb%d" % s)
            w = E // cuts
            nc.sync.dma_start(out=T[("a", s)][:, w * i:w * i + w], in_=af[P * s:P * s + P, w * i:w * i + w])

        def ld_raw(kind, a, c, i=0, cuts=1):
            if ("raw", kind, a, c) not in T:
                T[("raw", kind, a, c)] = rawp.tile([P, 4096], BF16, name="raw_%s%d%d" % (kind, a, c), tag="raw")
            t = T[("raw", kind, a, c)]
            if kind == "x":
                nc.sync.dma_start(
                    out=t[:].rearrange("p (s k) -> p s k", s=2),
                    in_=xf[256 * a:256 * a + 256, :].rearrange("(s p) k -> p s k", p=P),
                )
            else:
                W = Wg if kind == "g" else Wo
                tv = t[:].rearrange("p (j c) -> p j c", j=4)
                w = 1024 // cuts
                c0 = 1024 * a + w * i
                nc.sync.dma_start(
                    out=tv[:, :, w * i:w * i + w],
                    in_=W[512 * c:512 * c + 512, c0:c0 + w].rearrange("(p j) c -> p j c", j=4),
                )

        def vec_prep():
            nc.scalar.copy(
                out=vf[:].rearrange("p (t m) -> p t m", t=4), in_=vraw[:].rearrange("p (m t) -> p t m", t=4)
            )
            vt = psum.tile([P, 4, P], F32, name="vt", tag="ps")
            for t in range(4):
                nc.tensor.transpose(vt[:, t, :], vf[:, P * t:P * t + P], ident[:])
            nc.scalar.copy(out=vcol[:], in_=vt[:, :, 0:12])

        def bn(s):
            st = const.tile([P, 8, 6], F32, name="st%d" % s)
            T[("st", s)] = st
            for i in range(8):
                nc.vector.bn_stats(
                    out=st[:, i, :], in_=T[("a", s)][:, 256 * i:256 * i + 256].rearrange("p (g c) -> p c g", g=2)
                )

        def root(s):
            T[("std", s)] = const.tile([P, 8, 2], F32, name="std%d" % s)
            nc.scalar.activation(
                out=T[("std", s)][:], in_=T[("st", s)][:, :, 2:6:3], func=ACT.Sqrt, bias=eps_t[:, 0:1], scale=1.0 / P
            )

        def recip(s):
            T[("rstd", s)] = const.tile([P, 8, 2], F32, name="rstd%d" % s)
            nc.vector.reciprocal(out=T[("rstd", s)][:], in_=T[("std", s)][:])

        def x_transpose(g, sp):
            xt = psum.tile([P, 2, 256], F32, name="xt%d%d" % (g, sp), tag="ps")
            T[("xt", g, sp)] = xt
            xw = T[("raw", "x", sp, 0)][:].bitcast(F32)
            for u in range(2):
                for sl in range(2):
                    c0 = 1024 * sl + 256 * g
                    nc.tensor.transpose(xt[:, u, P * sl:P * sl + P], xw[:, c0 + u:c0 + 256:2], ident[:])

        def x_evac(g, sp):
            if ("xq", g) not in T:
                T[("xq", g)] = grpp.tile([P, 2048], BF16, name="xq%d" % g, tag="grp", align_bytes=64)
            xq32 = T[("xq", g)][:].bitcast(F32)[:, 512 * sp:512 * sp + 512]
            nc.scalar.copy(
                out=xq32.rearrange("p (r i u) -> p r u i", i=2, u=2),
                in_=T[("xt", g, sp)][:].rearrange("p u (r i) -> p r u i", i=2),
            )

        def unit_views(eng, kind, blk, c):
            raw = T[("raw", kind, blk // 2, c)]
            col0 = 512 * (blk % 2)
            src = raw[:].rearrange("p (j c) -> p j c", j=4)[:, :, col0:col0 + 512]
            if ("g4", kind, blk, c) not in T:
                pool = grpv if eng == "V" else grpp
                T[("g4", kind, blk, c)] = pool.tile(
                    [P, 2048], BF16, name="g4_%s%d%d" % (kind, blk, c), tag="grp", align_bytes=64
                )
            g4 = T[("g4", kind, blk, c)]
            if kind == "g":
                return (
                    g4[:].rearrange("p (t m j) -> p m j t", t=4, j=4),
                    src.rearrange("p j (m t) -> p m j t", t=4),
                )
            return g4[:].rearrange("p (c i j) -> p c j i", i=4, j=4), src.rearrange("p j (c i) -> p c j i", i=4)

        def regroup(eng, kind, blk, c):
            dst, src = unit_views(eng, kind, blk, c)
            if eng == "V":
                nc.vector.tensor_copy(out=dst, in_=src)
            else:
                nc.scalar.copy(out=dst, in_=src)

        def tensor_pass(kind, blk, c):
            raw = T[("raw", kind, blk // 2, c)]
            src = raw[:].rearrange("p (j c) -> p j c", j=4)[:, :, 512 * (blk % 2):512 * (blk % 2) + 512]
            for h in range(2):
                pt = psum.tile([P, 1024], BF16, name="pt_%s%d%d%d" % (kind, blk, c, h), tag="ps")
                T[("pt", kind, blk, c, h)] = pt
                for j in range(4):
                    mov = src[:, j, 256 * h:256 * h + 256]
                    if kind == "g":
                        dst = pt[:].rearrange("p (t m j) -> p j m t", t=4, j=4)[:, j]
                        mov = mov.rearrange("p (m t) -> p m t", t=4)
                    else:
                        dst = pt[:].rearrange("p (c j) -> p j c", j=4)[:, j]
                    nc.tensor.matmul(dst, lhsT=identb[:], rhs=mov, start=True, stop=True)

        def tensor_pass_out(kind, blk, c):
            g4 = grpp.tile([P, 2048], BF16, name="g4_%s%d%d" % (kind, blk, c), tag="grp", align_bytes=64)
            T[("g4", kind, blk, c)] = g4
            for h in range(2):
                pt = T[("pt", kind, blk, c, h)]
                if kind == "g":
                    nc.scalar.copy(
                        out=g4[:].rearrange("p (t r) -> p t r", t=4)[:, :, 256 * h:256 * h + 256],
                        in_=pt[:].rearrange("p (t r) -> p t r", t=4),
                    )
                else:
                    nc.scalar.copy(out=g4[:, 1024 * h:1024 * h + 1024], in_=pt[:])

        def quant(kind, blk, c):
            if ("wc", kind, blk) not in T:
                T[("wc", kind, blk)] = codep.tile(
                    [P, NPASS, 512], U32, name="wc_%s%d" % (kind, blk), tag="wc", align_bytes=64
                )
                T[("ws", kind, blk)] = codep.tile(
                    [P, NPASS, 512], U8, name="ws_%s%d" % (kind, blk), tag="ws", align_bytes=64
                )
            nc.vector.quantize_mx(
                out=T[("wc", kind, blk)][:, c, :].bitcast(FP8X4),
                scales=T[("ws", kind, blk)][:, c, :],
                in_=T[("g4", kind, blk, c)][:],
            )

        def mx1(G, t):
            z = psum.tile([P, S], F32, name="z%d%d" % (G, t), tag="ps")
            T[("z", G, t)] = z
            wc, ws = T[("wc", "g", G)], T[("ws", "g", G)]
            for c in range(NPASS):
                nc.tensor.matmul_mx(
                    out=z[:],
                    lhsT=wc[:, c, P * t:P * t + P].bitcast(FP8X4),
                    lhsT_scale=ws[:, c, P * t:P * t + P],
                    rhs=xc[:, c, :].bitcast(FP8X4),
                    rhs_scale=xs[:, c, :],
                    start=(c == 0),
                    stop=(c == NPASS - 1),
                )

        def normalise(G, s):
            nrm = normp.tile([P, 512], F32, name="nrm%d%d" % (G, s), tag="nrm")
            T[("nrm", G, s)] = nrm
            for q in range(4):
                gi = 4 * G + q
                i, e = gi // 2, gi % 2
                nc.vector.tensor_scalar(
                    out=nrm[:].rearrange("p (t m) -> p t m", t=4)[:, :, 32 * q:32 * q + 32],
                    in0=T[("a", s)][:, P * gi:P * gi + P].rearrange("p (m t) -> p t m", t=4),
                    scalar1=T[("st", s)][:, i, 1 + 3 * e:2 + 3 * e],
                    scalar2=T[("rstd", s)][:, i, e:e + 1],
                    op0=ALU.subtract,
                    op1=ALU.mult,
                )

        def n_transpose(G, t):
            nT = psum.tile([P, S], F32, name="nT%d%d" % (G, t), tag="ps")
            T[("nT", G, t)] = nT
            for s in range(4):
                nc.tensor.transpose(nT[:, P * s:P * s + P], T[("nrm", G, s)][:, P * t:P * t + P], ident[:])

        def silu(G, t):
            if ("sil", G) not in T:
                T[("sil", G)] = gatep.tile([P, 2048], F32, name="sil%d" % G, tag="sil")
            nc.scalar.activation(
                out=T[("sil", G)][:, S * t:S * t + S], in_=T[("z", G, t)][:], func=ACT.Silu,
                bias=vcol[:, t, G:G + 1], scale=1.0,
            )

        def gain(G, t):
            if ("gw", G) not in T:
                T[("gw", G)] = gatep.tile([P, 2048], F32, name="gw%d" % G, tag="gw")
            nc.scalar.activation(
                out=T[("gw", G)][:, S * t:S * t + S], in_=T[("nT", G, t)][:], func=ACT.Identity,
                bias=vcol[:, t, 8 + G:9 + G], scale=vcol[:, t, 4 + G:5 + G],
            )

        def gate_mul(G):
            hq = grpv.tile([P, 2048], BF16, name="hq%d" % G, tag="grp", align_bytes=64)
            T[("hq", G)] = hq
            nc.vector.tensor_tensor(
                out=hq[:].rearrange("p (c i t) -> p c t i", i=4, t=4),
                in0=T[("sil", G)][:].rearrange("p (t c i) -> p c t i", t=4, i=4),
                in1=T[("gw", G)][:].rearrange("p (t c i) -> p c t i", t=4, i=4),
                op=ALU.mult,
            )

        def mx2(NB, G):
            if G == 0:
                for s in range(4):
                    T[("acc", NB, s)] = psum.tile([P, 512], F32, name="acc%d%d" % (NB, s), tag="ps")
            wc, ws = T[("wc", "o", NB)], T[("ws", "o", NB)]
            for s in range(4):
                nc.tensor.matmul_mx(
                    out=T[("acc", NB, s)][:],
                    lhsT=hc[:, G, P * s:P * s + P].bitcast(FP8X4),
                    lhsT_scale=hs[:, G, P * s:P * s + P],
                    rhs=wc[:, G, :].bitcast(FP8X4),
                    rhs_scale=ws[:, G, :],
                    start=(G == 0),
                    stop=(G == NPASS - 1),
                )

        def bias_out(NB, s):
            o_sb = outp.tile([P, 512], F32, name="o%d%d" % (NB, s), tag="o")
            T[("o", NB, s)] = o_sb
            nc.vector.tensor_tensor(
                out=o_sb[:], in0=T[("acc", NB, s)][:], in1=bo_bc[:, 512 * NB:512 * NB + 512], op=ALU.add
            )

        vec_prep()
        for tok in pipeline():
            k, arg = tok[0], tok[1:]
            if k == "ldA":
                ld_attn(*arg)
            elif k == "ld":
                ld_raw(*arg)
            elif k == "ldbo":
                nc.sync.dma_start(out=bo_bc[:], in_=bo.partition_broadcast(P))
            elif k == "bn":
                bn(*arg)
            elif k == "sqrt":
                root(*arg)
            elif k == "recip":
                recip(*arg)
            elif k == "PI":
                tensor_pass(*arg)
            elif k == "PE":
                tensor_pass_out(*arg)
            elif k == "xT":
                x_transpose(*arg)
            elif k == "XE":
                x_evac(*arg)
            elif k == "Qx":
                nc.vector.quantize_mx(
                    out=xc[:, arg[0], :].bitcast(FP8X4), scales=xs[:, arg[0], :], in_=T[("xq", arg[0])][:]
                )
            elif k == "RGV":
                regroup("V", *arg)
            elif k == "RGS":
                regroup("S", *arg)
            elif k == "Q":
                quant(*arg)
            elif k == "MX1":
                mx1(*arg)
            elif k == "J4":
                normalise(*arg)
            elif k == "T":
                n_transpose(*arg)
            elif k == "SIL":
                silu(*arg)
            elif k == "GW":
                gain(*arg)
            elif k == "MUL":
                gate_mul(*arg)
            elif k == "QH":
                nc.vector.quantize_mx(
                    out=hc[:, arg[0], :].bitcast(FP8X4), scales=hs[:, arg[0], :], in_=T[("hq", arg[0])][:]
                )
            elif k == "MX2":
                mx2(*arg)
            elif k == "J5":
                bias_out(*arg)
            elif k == "E5a":
                NB, s = arg
                T[("o", NB, s)] = outp.tile([P, 512], F32, name="o%d%d" % (NB, s), tag="o")
                nc.scalar.copy(out=T[("o", NB, s)][:], in_=T[("acc", NB, s)][:])
            elif k == "E5b":
                NB, s = arg
                o_sb = T[("o", NB, s)]
                nc.gpsimd.tensor_tensor(
                    out=o_sb[:], in0=o_sb[:], in1=bo_bc[:, 512 * NB:512 * NB + 512], op=ALU.add
                )
            elif k == "st":
                NB, s = arg
                nc.sync.dma_start(out=of[P * s:P * s + P, 512 * NB:512 * NB + 512], in_=T[("o", NB, s)][:])
            else:
                assert False, k
